import numpy as np
import ml_dtypes


def mxq(x, axis, fmt="e4m3"):
    dtype, down = {"e4m3": (ml_dtypes.float8_e4m3fn, 7), "e5m2": (ml_dtypes.float8_e5m2, 14)}[fmt]
    v = np.moveaxis(np.asarray(x, np.float32).astype(ml_dtypes.bfloat16).astype(np.float64), axis, -1)
    blocks = v.reshape(v.shape[:-1] + (-1, 32))
    amax = np.abs(blocks).max(-1, keepdims=True)
    byte = np.maximum(np.where(amax > 0, np.frexp(amax)[1] - 1 + 127, 0) - down, 1)
    scale = np.exp2(byte - 127.0)
    codes = (blocks / scale).astype(np.float32).astype(dtype).astype(np.float64)
    return np.moveaxis((codes * scale).reshape(v.shape), -1, axis)


WIDE = False


def mx_kscale(k):
    if not WIDE:
        return np.ones(k)
    levels = np.array([10, -10, 5, -5, 0])
    a = np.random.permutation(np.resize(levels, k // 512 * 4)).reshape(k // 512, 4)
    idx = np.arange(k)
    return np.exp2(a[idx // 512, idx % 128 // 32])


BF16 = ml_dtypes.bfloat16


def bf(x):
    return np.asarray(x, np.float32).astype(BF16)


def f64(x):
    return np.asarray(x).astype(np.float64)


E2M1 = np.array([0.0, 0.5, 1.0, 1.5, 2.0, 3.0, 4.0, 6.0, -0.0, -0.5, -1.0, -1.5, -2.0, -3.0, -4.0, -6.0])


def pack_weight(w, fmt):
    k, n = w.shape
    w = f64(bf(w)).reshape(k // 32, 32, n)
    amax = np.abs(w).max(1)
    if fmt == "e4m3":
        byte = np.frexp(amax)[1] - 1 + 127 - 7
    else:
        mant, ex = np.frexp(amax / 6.0)
        byte = np.where(mant > 0.5, ex, ex - 1) + 127
    byte = np.clip(np.where(amax > 0, byte, 1), 1, 254)
    scaled = (w * np.exp2(127.0 - byte)[:, None, :]).reshape(k, n).astype(np.float32)
    by_word = np.ascontiguousarray(scaled.reshape(k // 512, 128, 4, n).transpose(0, 1, 3, 2))
    if fmt == "e4m3":
        words = by_word.astype(ml_dtypes.float8_e4m3fn).view(np.uint8)
    else:
        c = by_word.astype(ml_dtypes.float4_e2m1fn).view(np.uint8) & 0xF
        words = c[..., 0::2] | (c[..., 1::2] << 4)
    return np.ascontiguousarray(words), np.ascontiguousarray(byte.astype(np.uint8).reshape(k // 512, 16, n))


def unpack_weight(words, scales, fmt):
    g, p, n, _ = words.shape
    if fmt == "e4m3":
        vals = np.ascontiguousarray(words).view(ml_dtypes.float8_e4m3fn).astype(np.float64)
    else:
        nib = np.empty((g, p, n, 4), np.uint8)
        nib[..., 0::2] = words & 0xF
        nib[..., 1::2] = words >> 4
        vals = E2M1[nib]
    vals = vals * np.repeat(np.exp2(scales.astype(np.float64) - 127.0), 8, axis=1)[..., None]
    return vals.transpose(0, 1, 3, 2).reshape(g * 512, n)


N, E, SD, AD, RD, HID, NH = 4096, 3, 120, 8, 8, 512, 3
OD = SD + RD
FMT = "e4m3"


def swish(v):
    return v * (1.0 / (1.0 + np.exp(-v)))


def softplus(v):
    return np.maximum(v, 0.0) + np.log1p(np.exp(-np.abs(v)))


def soft_clamp_exp(v, hi, lo):
    v = (hi - softplus(hi - 2.0 * v)) / 2.0
    v = (lo + softplus(2.0 * v - lo)) / 2.0
    return np.exp(v)


def setup_inputs():
    ks = mx_kscale(HID)
    h = bf(swish(np.random.standard_normal((N, E, HID))) * ks)
    Wh = np.random.standard_normal((E, HID, HID)) * 1.6 / np.sqrt(HID) / ks[None, :, None]
    Wh_words, Wh_scales = pack_weight(Wh.reshape(-1, HID), FMT)
    bh = bf(np.random.standard_normal((E, HID)) * 0.2)
    Wmu = np.random.standard_normal((E, HID, OD)) * 1.6 / np.sqrt(HID)
    Wmu_words, Wmu_scales = pack_weight(Wmu.reshape(-1, OD), FMT)
    bmu = bf(np.random.standard_normal((E, OD)) * 0.3)
    Wsig = np.random.standard_normal((E, HID, OD)) * 2.0 / np.sqrt(HID)
    Wsig_words, Wsig_scales = pack_weight(Wsig.reshape(-1, OD), FMT)
    bsig = bf(np.random.standard_normal((E, OD)) * 0.3)
    return {"h": h,
            "Wh_words": Wh_words,
            "Wh_scales": Wh_scales,
            "bh": bh,
            "Wmu_words": Wmu_words,
            "Wmu_scales": Wmu_scales,
            "bmu": bmu,
            "Wsig_words": Wsig_words,
            "Wsig_scales": Wsig_scales,
            "bsig": bsig,
            "max_lv_s": bf(0.5 + 0.2 * np.random.standard_normal((1, SD))),
            "min_lv_s": bf(-2.5 + 0.3 * np.random.standard_normal((1, SD))),
            "max_lv_r": bf(0.5 + 0.2 * np.random.standard_normal((1, RD))),
            "min_lv_r": bf(-2.5 + 0.3 * np.random.standard_normal((1, RD)))}


def reference(h, Wh_words, Wh_scales, bh, Wmu_words, Wmu_scales, bmu, Wsig_words, Wsig_scales, bsig, max_lv_s, min_lv_s, max_lv_r, min_lv_r):
    hq = mxq(f64(h), 2, "e4m3").transpose(1, 0, 2)
    g = swish((hq @ unpack_weight(Wh_words, Wh_scales, FMT).reshape(E, HID, HID)) + f64(bh)[:, None, :])
    gq = mxq(g, 2, "e4m3")
    mu = ((gq @ unpack_weight(Wmu_words, Wmu_scales, FMT).reshape(E, HID, OD)) + f64(bmu)[:, None, :]).transpose(1, 0, 2)
    sigma = ((gq @ unpack_weight(Wsig_words, Wsig_scales, FMT).reshape(E, HID, OD)) + f64(bsig)[:, None, :]).transpose(1, 0, 2)
    ds_mu, r_mu = mu[..., :SD], mu[..., SD:]
    ds_sg, r_sg = sigma[..., :SD], sigma[..., SD:]
    ds_sg = soft_clamp_exp(ds_sg, f64(max_lv_s), f64(min_lv_s))
    r_sg = soft_clamp_exp(r_sg, f64(max_lv_r), f64(min_lv_r))
    return ds_mu, ds_sg, r_mu, r_sg

@@ -1,0 +1,319 @@
+from contextlib import ExitStack
+
+import concourse.mybir as mybir
+from concourse.masks import make_identity
+
+F32 = mybir.dt.float32
+BF16 = mybir.dt.bfloat16
+I32 = mybir.dt.int32
+U32 = mybir.dt.uint32
+U8 = mybir.dt.uint8
+FP8X4 = mybir.dt.float8_e4m3fn_x4
+ACT = mybir.ActivationFunctionType
+ALU = mybir.AluOpType
+
+P = 128
+PACK = 4
+MEMBERS = 3
+HID = 512
+OUT = 128
+STATE = 120
+BLOCKS = 96
+ROUND = 2
+ROUNDS = BLOCKS // ROUND
+LOAD_BLOCKS = 6
+STORE_BLOCKS = 8
+SQRT_BLOCKS = 4
+
+FLOPS = 2 * 4096 * MEMBERS * (HID * HID + 2 * HID * OUT)
+
+
+def load_weight(nc, pool, words_dram, scales_dram, width, label):
+    words = pool.tile([P, MEMBERS, PACK * width], U8, name=label + "_words", align_bytes=64)
+    planes = pool.tile([P, MEMBERS, width], U8, name=label + "_planes", align_bytes=64)
+    nc.vector.memset(planes[:].bitcast(I32), 0)
+    for quadrant in range(4):
+        nc.sync.dma_start(
+            out=planes[32 * quadrant : 32 * quadrant + 4].bitcast(I32),
+            in_=scales_dram[:, 4 * quadrant : 4 * quadrant + 4, :].rearrange("e r n -> r e n").bitcast(I32),
+        )
+    nc.sync.dma_start(
+        out=words[:].bitcast(I32),
+        in_=words_dram.rearrange("e p n t -> p e (n t)").bitcast(I32),
+    )
+    return words, planes
+
+
+def tile_ensembleenvprob_pa_t_e_kernel(
+    tc,
+    h,
+    Wh_words,
+    Wh_scales,
+    bh,
+    Wmu_words,
+    Wmu_scales,
+    bmu,
+    Wsig_words,
+    Wsig_scales,
+    bsig,
+    max_lv_s,
+    min_lv_s,
+    max_lv_r,
+    min_lv_r,
+    out_0,
+    out_1,
+    out_2,
+    out_3,
+):
+    nc = tc.nc
+    h_blocks = h.flatten_outer_dims().rearrange("(p b) k -> p b k", b=BLOCKS)
+    ds_mu = out_0.flatten_outer_dims().rearrange("(p b) o -> p b o", b=BLOCKS)
+    ds_sg = out_1.flatten_outer_dims().rearrange("(p b) o -> p b o", b=BLOCKS)
+    r_mu = out_2.flatten_outer_dims().rearrange("(p b) o -> p b o", b=BLOCKS)
+    r_sg = out_3.flatten_outer_dims().rearrange("(p b) o -> p b o", b=BLOCKS)
+
+    def store_blocks(staged, first_block, state_out, reward_out):
+        blocks = slice(first_block, first_block + STORE_BLOCKS)
+        nc.sync.dma_start(out=state_out[:, blocks, :], in_=staged[:, :, 0:STATE])
+        nc.sync.dma_start(out=reward_out[:, blocks, :], in_=staged[:, :, STATE:OUT])
+
+    with ExitStack() as stack:
+        stack.enter_context(tc.manual_schedule())
+        keep = stack.enter_context(tc.tile_pool(name="keep", bufs=1))
+        work = stack.enter_context(tc.tile_pool(name="work", bufs=2))
+        results = stack.enter_context(tc.tile_pool(name="results", bufs=4))
+
+        ident = keep.tile([P, P], F32)
+        make_identity(nc, ident[:])
+
+        h_tiles = []
+        for c in range(BLOCKS // LOAD_BLOCKS):
+            h_tiles.append(keep.tile([P, LOAD_BLOCKS, HID], BF16, name="h%d" % c))
+
+        def load_h(c):
+            nc.sync.dma_start(out=h_tiles[c][:], in_=h_blocks[:, c * LOAD_BLOCKS : (c + 1) * LOAD_BLOCKS, :])
+
+        load_h(0)
+        wh_words, wh_planes = load_weight(nc, keep, Wh_words, Wh_scales, HID, "wh")
+        load_h(1)
+        wmu_words, wmu_planes = load_weight(nc, keep, Wmu_words, Wmu_scales, OUT, "wmu")
+        wsig_words, wsig_planes = load_weight(nc, keep, Wsig_words, Wsig_scales, OUT, "wsig")
+        for c in range(2, BLOCKS // LOAD_BLOCKS):
+            load_h(c)
+
+        rows_bf = keep.tile([P, P], BF16)
+        nc.vector.memset(rows_bf[:], 0.0)
+        nc.scalar.dma_start(out=rows_bf[0:MEMBERS, :], in_=bsig)
+        nc.scalar.dma_start(out=rows_bf[3:4, 0:STATE], in_=max_lv_s)
+        nc.scalar.dma_start(out=rows_bf[4:5, STATE:OUT], in_=max_lv_r)
+        nc.scalar.dma_start(out=rows_bf[5:6, 0:STATE], in_=min_lv_s)
+        nc.scalar.dma_start(out=rows_bf[6:7, STATE:OUT], in_=min_lv_r)
+        bh_bf = keep.tile([P, MEMBERS * HID], BF16)
+        nc.scalar.dma_start(out=bh_bf[:], in_=bh.rearrange("e k -> (e k)").partition_broadcast(P))
+        bmu_bf = keep.tile([P, MEMBERS, OUT], BF16)
+        nc.scalar.dma_start(
+            out=bmu_bf[:].rearrange("n e o -> n (e o)"),
+            in_=bmu.rearrange("e o -> (e o)").partition_broadcast(P),
+        )
+
+        tanh_all = keep.tile([P, BLOCKS, P], F32)
+
+        with tc.psum_pool(name="psum", bufs=1) as psum:
+            live = {}
+
+            def transpose_h(r):
+                hT = psum.tile([P, ROUND, 2, P], F32)
+                for g in range(ROUND):
+                    block = r * ROUND + g
+                    words = h_tiles[block // LOAD_BLOCKS][:, block % LOAD_BLOCKS, :].bitcast(F32)
+                    for u in range(2):
+                        nc.tensor.transpose(out=hT[:, g, u, :], in_=words[:, u : HID // 2 : 2], identity=ident[:])
+                live["hT", r] = hT
+
+            def regroup_h(r):
+                h_grouped = work.tile([P, ROUND, P, PACK], BF16, align_bytes=64)
+                nc.scalar.copy(out=h_grouped[:].bitcast(F32), in_=live["hT", r][:].rearrange("p g u n -> p g n u"))
+                live["h_grouped", r] = h_grouped
+
+            def quantise_h(r):
+                h_codes = work.tile([P, ROUND * P], U32, align_bytes=64)
+                h_scales = work.tile([P, ROUND * P], U8, align_bytes=64)
+                nc.vector.quantize_mx(
+                    out=h_codes[:].bitcast(FP8X4),
+                    scales=h_scales[:],
+                    in_=live["h_grouped", r][:].rearrange("p g n t -> p (g n t)"),
+                )
+                live["h_mx", r] = (h_codes, h_scales)
+
+            def layer_1(r):
+                h_codes, h_scales = live["h_mx", r]
+                for g in range(ROUND):
+                    e = (r * ROUND + g) % MEMBERS
+                    x_ps = psum.tile([P, HID], F32, tag="x_ps%d" % g)
+                    nc.tensor.matmul_mx(
+                        out=x_ps[:],
+                        lhsT=h_codes[:, g * P : (g + 1) * P].bitcast(FP8X4),
+                        lhsT_scale=h_scales[:, g * P : (g + 1) * P],
+                        rhs=wh_words[:, e, :].bitcast(FP8X4),
+                        rhs_scale=wh_planes[:, e, :],
+                        start=True,
+                        stop=True,
+                    )
+                    live["x_ps", r, g] = x_ps
+
+            def add_bh(r):
+                x_sb = work.tile([P, ROUND, PACK, P], F32)
+                for g in range(ROUND):
+                    e = (r * ROUND + g) % MEMBERS
+                    nc.vector.tensor_tensor(
+                        out=x_sb[:, g],
+                        in0=live["x_ps", r, g][:].rearrange("n (p t) -> n t p", t=PACK),
+                        in1=bh_tp[:, e],
+                        op=ALU.add,
+                    )
+                live["x_sb", r] = x_sb
+
+            def transpose_x(r):
+                x_sb = live["x_sb", r]
+                for g in range(ROUND):
+                    xT = psum.tile([P, PACK, P], F32, tag="xT%d" % g)
+                    for t in range(PACK):
+                        nc.tensor.transpose(out=xT[:, t, :], in_=x_sb[:, g, t, :], identity=ident[:])
+                    live["xT", r, g] = xT
+
+            def swish(r):
+                g_grouped = work.tile([P, ROUND, P, PACK], BF16, align_bytes=64)
+                for g in range(ROUND):
+                    nc.scalar.activation(
+                        out=g_grouped[:, g], in_=live["xT", r, g][:].rearrange("p t n -> p n t"), func=ACT.Silu
+                    )
+                live["g_grouped", r] = g_grouped
+
+            def quantise_g(r):
+                g_codes = work.tile([P, ROUND * P], U32, align_bytes=64)
+                g_scales = work.tile([P, ROUND * P], U8, align_bytes=64)
+                nc.vector.quantize_mx(
+                    out=g_codes[:].bitcast(FP8X4),
+                    scales=g_scales[:],
+                    in_=live["g_grouped", r][:].rearrange("p g n t -> p (g n t)"),
+                )
+                live["g_mx", r] = (g_codes, g_scales)
+
+            def heads(r):
+                g_codes, g_scales = live["g_mx", r]
+                mu_ps = psum.tile([P, ROUND, OUT], F32)
+                sigT_ps = psum.tile([P, ROUND, P], F32)
+                for g in range(ROUND):
+                    e = (r * ROUND + g) % MEMBERS
+                    rows = slice(g * P, (g + 1) * P)
+                    nc.tensor.matmul_mx(
+                        out=mu_ps[:, g, :],
+                        lhsT=g_codes[:, rows].bitcast(FP8X4),
+                        lhsT_scale=g_scales[:, rows],
+                        rhs=wmu_words[:, e, :].bitcast(FP8X4),
+                        rhs_scale=wmu_planes[:, e, :],
+                        start=True,
+                        stop=True,
+                    )
+                    nc.tensor.matmul_mx(
+                        out=sigT_ps[:, g, :],
+                        lhsT=wsig_words[:, e, :].bitcast(FP8X4),
+                        lhsT_scale=wsig_planes[:, e, :],
+                        rhs=g_codes[:, rows].bitcast(FP8X4),
+                        rhs_scale=g_scales[:, rows],
+                        start=True,
+                        stop=True,
+                    )
+                live["mu_ps", r] = mu_ps
+                live["sigT_ps", r] = sigT_ps
+
+            def tanh_sigma(r):
+                sigT_ps = live["sigT_ps", r]
+                for g in range(ROUND):
+                    block = r * ROUND + g
+                    e = block % MEMBERS
+                    nc.scalar.activation(
+                        out=tanh_all[:, block, :], in_=sigT_ps[:, g, :], func=ACT.Tanh, bias=tanh_bias[:, e : e + 1]
+                    )
+
+            def add_bmu(r):
+                first = r * ROUND
+                place = first % STORE_BLOCKS
+                if place == 0:
+                    staged = results.tile([P, STORE_BLOCKS, OUT], F32)
+                    live["mu_sb"] = staged
+                mu_sb = live["mu_sb"]
+                e = first % MEMBERS
+                nc.vector.tensor_tensor(
+                    out=mu_sb[:, place : place + ROUND, :],
+                    in0=live["mu_ps", r][:],
+                    in1=bmu_cycle[:, e : e + ROUND, :],
+                    op=ALU.add,
+                )
+                if place + ROUND == STORE_BLOCKS:
+                    store_blocks(mu_sb, first + ROUND - STORE_BLOCKS, ds_mu, r_mu)
+
+            def run(stage, r):
+                if 0 <= r < ROUNDS:
+                    stage(r)
+
+            transpose_h(0)
+            regroup_h(0)
+            quantise_h(0)
+
+            rows_f32 = keep.tile([P, P], F32)
+            nc.vector.tensor_copy(out=rows_f32[:], in_=rows_bf[:])
+            cols_ps = psum.tile([P, P], F32)
+            nc.tensor.transpose(out=cols_ps[:], in_=rows_f32[:], identity=ident[:])
+            cols = keep.tile([P, 8], F32)
+            nc.vector.tensor_copy(out=cols[:], in_=cols_ps[:, 0:8])
+            hi_lo = keep.tile([P, 2], F32)
+            nc.vector.tensor_tensor(out=hi_lo[:], in0=cols[:, 3:6:2], in1=cols[:, 4:7:2], op=ALU.add)
+            exp_hi_lo = keep.tile([P, 2], F32)
+            nc.scalar.activation(out=exp_hi_lo[:], in_=hi_lo[:], func=ACT.Exp)
+            sqrt_scale = keep.tile([P, 1], F32)
+            nc.vector.tensor_scalar(out=sqrt_scale[:], in0=exp_hi_lo[:, 0:1], scalar1=0.5, scalar2=None, op0=ALU.mult)
+            sqrt_bias = keep.tile([P, 1], F32)
+            nc.vector.tensor_tensor(out=sqrt_bias[:], in0=sqrt_scale[:], in1=exp_hi_lo[:, 1:2], op=ALU.add)
+            half_hi = keep.tile([P, 1], F32)
+            nc.vector.tensor_scalar(out=half_hi[:], in0=hi_lo[:, 0:1], scalar1=0.5, scalar2=None, op0=ALU.mult)
+            tanh_bias = keep.tile([P, MEMBERS], F32)
+            nc.vector.tensor_scalar(
+                out=tanh_bias[:], in0=cols[:, 0:MEMBERS], scalar1=half_hi[:, 0:1], scalar2=None, op0=ALU.subtract
+            )
+            bh_tp = keep.tile([P, MEMBERS, PACK, P], F32)
+            nc.vector.tensor_copy(out=bh_tp[:], in_=bh_bf[:].rearrange("n (e p t) -> n e t p", e=MEMBERS, t=PACK))
+            bmu_cycle = keep.tile([P, MEMBERS + ROUND - 1, OUT], F32)
+            nc.vector.tensor_copy(out=bmu_cycle[:, 0:MEMBERS, :], in_=bmu_bf[:])
+            nc.vector.tensor_copy(out=bmu_cycle[:, MEMBERS:, :], in_=bmu_bf[:, 0 : ROUND - 1, :])
+
+            for i in range(1, ROUNDS + 4):
+                run(tanh_sigma, i - 4)
+                run(quantise_g, i - 3)
+                run(add_bmu, i - 4)
+                run(transpose_h, i)
+                run(regroup_h, i)
+                run(quantise_h, i)
+                run(transpose_x, i - 2)
+                run(swish, i - 2)
+                run(layer_1, i - 1)
+                run(add_bh, i - 1)
+                run(heads, i - 3)
+
+        with tc.psum_pool(name="psum_sg", bufs=4) as psum_sg:
+            for first in range(0, BLOCKS, STORE_BLOCKS):
+                sg_sb = results.tile([P, STORE_BLOCKS, OUT], F32, tag="staged")
+                for part in range(0, STORE_BLOCKS, SQRT_BLOCKS):
+                    sgT = work.tile([P, SQRT_BLOCKS, P], F32)
+                    nc.scalar.activation(
+                        out=sgT[:],
+                        in_=tanh_all[:, first + part : first + part + SQRT_BLOCKS, :],
+                        func=ACT.Sqrt,
+                        bias=sqrt_bias[:, 0:1],
+                        scale=sqrt_scale[:, 0:1],
+                    )
+                    sg_ps = psum_sg.tile([P, SQRT_BLOCKS, OUT], F32)
+                    for g in range(SQRT_BLOCKS):
+                        nc.tensor.transpose(out=sg_ps[:, g, :], in_=sgT[:, g, :], identity=ident[:])
+                    nc.vector.tensor_copy(out=sg_sb[:, part : part + SQRT_BLOCKS, :], in_=sg_ps[:])
+                store_blocks(sg_sb, first, ds_sg, r_sg)

@@ -162,7 +162,7 @@ def tile_ensembleenvprob_pa_t_e_kernel(
                     live["x_ps", r, g] = x_ps
 
             def add_bh(r):
-                x_sb = work.tile([P, ROUND, PACK, P], F32)
+                x_sb = work.tile([P, ROUND, PACK, P], F32, bufs=3)
                 for g in range(ROUND):
                     e = (r * ROUND + g) % MEMBERS
                     nc.vector.tensor_tensor(
@@ -287,18 +287,18 @@ def tile_ensembleenvprob_pa_t_e_kernel(
             nc.vector.tensor_copy(out=bmu_cycle[:, 0:MEMBERS, :], in_=bmu_bf[:])
             nc.vector.tensor_copy(out=bmu_cycle[:, MEMBERS:, :], in_=bmu_bf[:, 0 : ROUND - 1, :])
 
-            for i in range(1, ROUNDS + 4):
-                run(tanh_sigma, i - 4)
-                run(quantise_g, i - 3)
-                run(add_bmu, i - 4)
+            for i in range(1, ROUNDS + 6):
+                run(tanh_sigma, i - 5)
+                run(quantise_g, i - 4)
+                run(add_bmu, i - 5)
                 run(transpose_h, i)
                 run(regroup_h, i)
                 run(quantise_h, i)
-                run(transpose_x, i - 2)
-                run(swish, i - 2)
+                run(transpose_x, i - 3)
+                run(swish, i - 3)
                 run(layer_1, i - 1)
                 run(add_bh, i - 1)
-                run(heads, i - 3)
+                run(heads, i - 4)
 
         with tc.psum_pool(name="psum_sg", bufs=4) as psum_sg:
             for first in range(0, BLOCKS, STORE_BLOCKS):

@@ -18,11 +18,13 @@ MEMBERS = 3
 HID = 512
 OUT = 128
 STATE = 120
+REWARD = OUT - STATE
 BLOCKS = 96
 ROUND = 2
 ROUNDS = BLOCKS // ROUND
-LOAD_BLOCKS = 6
-STORE_BLOCKS = 8
+GROUP = ROUND * MEMBERS
+STORE_BLOCKS = 2 * GROUP
+STORE_ROUNDS = STORE_BLOCKS // ROUND
 SQRT_BLOCKS = 4
 
 FLOPS = 2 * 4096 * MEMBERS * (HID * HID + 2 * HID * OUT)
@@ -72,33 +74,34 @@ def tile_ensembleenvprob_pa_t_e_kernel(
     r_mu = out_2.flatten_outer_dims().rearrange("(p b) o -> p b o", b=BLOCKS)
     r_sg = out_3.flatten_outer_dims().rearrange("(p b) o -> p b o", b=BLOCKS)
 
-    def store_blocks(staged, first_block, state_out, reward_out):
-        blocks = slice(first_block, first_block + STORE_BLOCKS)
-        nc.sync.dma_start(out=state_out[:, blocks, :], in_=staged[:, :, 0:STATE])
-        nc.sync.dma_start(out=reward_out[:, blocks, :], in_=staged[:, :, STATE:OUT])
+    def blocks_from(first):
+        return slice(first, first + MEMBERS * (ROUND - 1) + 1, MEMBERS)
+
+    def first_block(r):
+        return GROUP * (r // MEMBERS) + r % MEMBERS
 
     with ExitStack() as stack:
         stack.enter_context(tc.manual_schedule())
         keep = stack.enter_context(tc.tile_pool(name="keep", bufs=1))
         work = stack.enter_context(tc.tile_pool(name="work", bufs=2))
-        results = stack.enter_context(tc.tile_pool(name="results", bufs=4))
+        results = stack.enter_context(tc.tile_pool(name="results", bufs=3))
 
         ident = keep.tile([P, P], F32)
         make_identity(nc, ident[:])
 
         h_tiles = []
-        for c in range(BLOCKS // LOAD_BLOCKS):
-            h_tiles.append(keep.tile([P, LOAD_BLOCKS, HID], BF16, name="h%d" % c))
+        for c in range(BLOCKS // GROUP):
+            h_tiles.append(keep.tile([P, GROUP, HID], BF16, name="h%d" % c))
 
         def load_h(c):
-            nc.sync.dma_start(out=h_tiles[c][:], in_=h_blocks[:, c * LOAD_BLOCKS : (c + 1) * LOAD_BLOCKS, :])
+            nc.sync.dma_start(out=h_tiles[c][:], in_=h_blocks[:, c * GROUP : (c + 1) * GROUP, :])
 
         load_h(0)
         wh_words, wh_planes = load_weight(nc, keep, Wh_words, Wh_scales, HID, "wh")
         load_h(1)
         wmu_words, wmu_planes = load_weight(nc, keep, Wmu_words, Wmu_scales, OUT, "wmu")
         wsig_words, wsig_planes = load_weight(nc, keep, Wsig_words, Wsig_scales, OUT, "wsig")
-        for c in range(2, BLOCKS // LOAD_BLOCKS):
+        for c in range(2, BLOCKS // GROUP):
             load_h(c)
 
         rows_bf = keep.tile([P, P], BF16)
@@ -117,6 +120,8 @@ def tile_ensembleenvprob_pa_t_e_kernel(
         )
 
         tanh_all = keep.tile([P, BLOCKS, P], F32)
+        mu_reward = keep.tile([P, BLOCKS, REWARD], F32)
+        sg_reward = keep.tile([P, BLOCKS, REWARD], F32)
 
         with tc.psum_pool(name="psum", bufs=1) as psum:
             live = {}
@@ -124,8 +129,7 @@ def tile_ensembleenvprob_pa_t_e_kernel(
             def transpose_h(r):
                 hT = psum.tile([P, ROUND, 2, P], F32)
                 for g in range(ROUND):
-                    block = r * ROUND + g
-                    words = h_tiles[block // LOAD_BLOCKS][:, block % LOAD_BLOCKS, :].bitcast(F32)
+                    words = h_tiles[r // MEMBERS][:, r % MEMBERS + MEMBERS * g, :].bitcast(F32)
                     for u in range(2):
                         nc.tensor.transpose(out=hT[:, g, u, :], in_=words[:, u : HID // 2 : 2], identity=ident[:])
                 live["hT", r] = hT
@@ -147,8 +151,8 @@ def tile_ensembleenvprob_pa_t_e_kernel(
 
             def layer_1(r):
                 h_codes, h_scales = live["h_mx", r]
+                e = r % MEMBERS
                 for g in range(ROUND):
-                    e = (r * ROUND + g) % MEMBERS
                     x_ps = psum.tile([P, HID], F32, tag="x_ps%d" % g)
                     nc.tensor.matmul_mx(
                         out=x_ps[:],
@@ -163,8 +167,8 @@ def tile_ensembleenvprob_pa_t_e_kernel(
 
             def add_bh(r):
                 x_sb = work.tile([P, ROUND, PACK, P], F32, bufs=3)
+                e = r % MEMBERS
                 for g in range(ROUND):
-                    e = (r * ROUND + g) % MEMBERS
                     nc.vector.tensor_tensor(
                         out=x_sb[:, g],
                         in0=live["x_ps", r, g][:].rearrange("n (p t) -> n t p", t=PACK),
@@ -201,57 +205,62 @@ def tile_ensembleenvprob_pa_t_e_kernel(
 
             def heads(r):
                 g_codes, g_scales = live["g_mx", r]
+                e = r % MEMBERS
                 mu_ps = psum.tile([P, ROUND, OUT], F32)
-                sigT_ps = psum.tile([P, ROUND, P], F32)
                 for g in range(ROUND):
-                    e = (r * ROUND + g) % MEMBERS
-                    rows = slice(g * P, (g + 1) * P)
                     nc.tensor.matmul_mx(
                         out=mu_ps[:, g, :],
-                        lhsT=g_codes[:, rows].bitcast(FP8X4),
-                        lhsT_scale=g_scales[:, rows],
+                        lhsT=g_codes[:, g * P : (g + 1) * P].bitcast(FP8X4),
+                        lhsT_scale=g_scales[:, g * P : (g + 1) * P],
                         rhs=wmu_words[:, e, :].bitcast(FP8X4),
                         rhs_scale=wmu_planes[:, e, :],
                         start=True,
                         stop=True,
                     )
-                    nc.tensor.matmul_mx(
-                        out=sigT_ps[:, g, :],
-                        lhsT=wsig_words[:, e, :].bitcast(FP8X4),
-                        lhsT_scale=wsig_planes[:, e, :],
-                        rhs=g_codes[:, rows].bitcast(FP8X4),
-                        rhs_scale=g_scales[:, rows],
-                        start=True,
-                        stop=True,
-                    )
+                sigT_ps = psum.tile([P, ROUND, P], F32)
+                nc.tensor.matmul_mx(
+                    out=sigT_ps[:].rearrange("o g n -> o (g n)"),
+                    lhsT=wsig_words[:, e, :].bitcast(FP8X4),
+                    lhsT_scale=wsig_planes[:, e, :],
+                    rhs=g_codes[:].bitcast(FP8X4),
+                    rhs_scale=g_scales[:],
+                    start=True,
+                    stop=True,
+                )
                 live["mu_ps", r] = mu_ps
                 live["sigT_ps", r] = sigT_ps
 
             def tanh_sigma(r):
-                sigT_ps = live["sigT_ps", r]
-                for g in range(ROUND):
-                    block = r * ROUND + g
-                    e = block % MEMBERS
-                    nc.scalar.activation(
-                        out=tanh_all[:, block, :], in_=sigT_ps[:, g, :], func=ACT.Tanh, bias=tanh_bias[:, e : e + 1]
-                    )
+                e = r % MEMBERS
+                nc.scalar.activation(
+                    out=tanh_all[:, blocks_from(first_block(r)), :],
+                    in_=live["sigT_ps", r][:],
+                    func=ACT.Tanh,
+                    bias=tanh_bias[:, e : e + 1],
+                )
 
             def add_bmu(r):
-                first = r * ROUND
-                place = first % STORE_BLOCKS
-                if place == 0:
-                    staged = results.tile([P, STORE_BLOCKS, OUT], F32)
-                    live["mu_sb"] = staged
-                mu_sb = live["mu_sb"]
-                e = first % MEMBERS
+                e = r % MEMBERS
+                if r % STORE_ROUNDS == 0:
+                    staged = results.tile([P, STORE_BLOCKS, STATE], F32)
+                    live["mu_state"] = staged
+                mu_state = live["mu_state"]
+                mu_ps = live["mu_ps", r]
                 nc.vector.tensor_tensor(
-                    out=mu_sb[:, place : place + ROUND, :],
-                    in0=live["mu_ps", r][:],
-                    in1=bmu_cycle[:, e : e + ROUND, :],
+                    out=mu_state[:, blocks_from(first_block(r) % STORE_BLOCKS), :],
+                    in0=mu_ps[:, :, 0:STATE],
+                    in1=bmu_f32[:, e : e + 1, 0:STATE].to_broadcast([P, ROUND, STATE]),
                     op=ALU.add,
                 )
-                if place + ROUND == STORE_BLOCKS:
-                    store_blocks(mu_sb, first + ROUND - STORE_BLOCKS, ds_mu, r_mu)
+                nc.vector.tensor_tensor(
+                    out=mu_reward[:, blocks_from(first_block(r)), :],
+                    in0=mu_ps[:, :, STATE:OUT],
+                    in1=bmu_f32[:, e : e + 1, STATE:OUT].to_broadcast([P, ROUND, REWARD]),
+                    op=ALU.add,
+                )
+                if r % STORE_ROUNDS == STORE_ROUNDS - 1:
+                    stored = r // STORE_ROUNDS * STORE_BLOCKS
+                    nc.sync.dma_start(out=ds_mu[:, stored : stored + STORE_BLOCKS, :], in_=mu_state[:])
 
             def run(stage, r):
                 if 0 <= r < ROUNDS:
@@ -283,9 +292,8 @@ def tile_ensembleenvprob_pa_t_e_kernel(
             )
             bh_tp = keep.tile([P, MEMBERS, PACK, P], F32)
             nc.vector.tensor_copy(out=bh_tp[:], in_=bh_bf[:].rearrange("n (e p t) -> n e t p", e=MEMBERS, t=PACK))
-            bmu_cycle = keep.tile([P, MEMBERS + ROUND - 1, OUT], F32)
-            nc.vector.tensor_copy(out=bmu_cycle[:, 0:MEMBERS, :], in_=bmu_bf[:])
-            nc.vector.tensor_copy(out=bmu_cycle[:, MEMBERS:, :], in_=bmu_bf[:, 0 : ROUND - 1, :])
+            bmu_f32 = keep.tile([P, MEMBERS, OUT], F32)
+            nc.vector.tensor_copy(out=bmu_f32[:], in_=bmu_bf[:])
 
             for i in range(1, ROUNDS + 6):
                 run(tanh_sigma, i - 5)
@@ -300,14 +308,17 @@ def tile_ensembleenvprob_pa_t_e_kernel(
                 run(add_bh, i - 1)
                 run(heads, i - 4)
 
+        nc.sync.dma_start(out=r_mu, in_=mu_reward[:])
+
         with tc.psum_pool(name="psum_sg", bufs=4) as psum_sg:
             for first in range(0, BLOCKS, STORE_BLOCKS):
-                sg_sb = results.tile([P, STORE_BLOCKS, OUT], F32, tag="staged")
+                sg_state = results.tile([P, STORE_BLOCKS, STATE], F32, tag="staged")
                 for part in range(0, STORE_BLOCKS, SQRT_BLOCKS):
+                    blocks = slice(first + part, first + part + SQRT_BLOCKS)
                     sgT = work.tile([P, SQRT_BLOCKS, P], F32)
                     nc.scalar.activation(
                         out=sgT[:],
-                        in_=tanh_all[:, first + part : first + part + SQRT_BLOCKS, :],
+                        in_=tanh_all[:, blocks, :],
                         func=ACT.Sqrt,
                         bias=sqrt_bias[:, 0:1],
                         scale=sqrt_scale[:, 0:1],
@@ -315,5 +326,7 @@ def tile_ensembleenvprob_pa_t_e_kernel(
                     sg_ps = psum_sg.tile([P, SQRT_BLOCKS, OUT], F32)
                     for g in range(SQRT_BLOCKS):
                         nc.tensor.transpose(out=sg_ps[:, g, :], in_=sgT[:, g, :], identity=ident[:])
-                    nc.vector.tensor_copy(out=sg_sb[:, part : part + SQRT_BLOCKS, :], in_=sg_ps[:])
-                store_blocks(sg_sb, first, ds_sg, r_sg)
+                    nc.vector.tensor_copy(out=sg_state[:, part : part + SQRT_BLOCKS, :], in_=sg_ps[:, :, 0:STATE])
+                    nc.vector.tensor_copy(out=sg_reward[:, blocks, :], in_=sg_ps[:, :, STATE:OUT])
+                nc.sync.dma_start(out=ds_sg[:, first : first + STORE_BLOCKS, :], in_=sg_state[:])
+            nc.sync.dma_start(out=r_sg, in_=sg_reward[:])

@@ -24,7 +24,6 @@ ROUND = 2
 ROUNDS = BLOCKS // ROUND
 GROUP = ROUND * MEMBERS
 STORE_BLOCKS = 2 * GROUP
-STORE_ROUNDS = STORE_BLOCKS // ROUND
 SQRT_BLOCKS = 4
 
 FLOPS = 2 * 4096 * MEMBERS * (HID * HID + 2 * HID * OUT)
@@ -120,7 +119,6 @@ def tile_ensembleenvprob_pa_t_e_kernel(
         )
 
         tanh_all = keep.tile([P, BLOCKS, P], F32)
-        mu_reward = keep.tile([P, BLOCKS, REWARD], F32)
         sg_reward = keep.tile([P, BLOCKS, REWARD], F32)
 
         with tc.psum_pool(name="psum", bufs=1) as psum:
@@ -241,26 +239,20 @@ def tile_ensembleenvprob_pa_t_e_kernel(
 
             def add_bmu(r):
                 e = r % MEMBERS
-                if r % STORE_ROUNDS == 0:
-                    staged = results.tile([P, STORE_BLOCKS, STATE], F32)
-                    live["mu_state"] = staged
-                mu_state = live["mu_state"]
-                mu_ps = live["mu_ps", r]
+                if e == 0:
+                    mu_group = results.tile([P, GROUP, OUT], F32, bufs=4)
+                    live["mu_sb"] = mu_group
+                mu_sb = live["mu_sb"]
                 nc.vector.tensor_tensor(
-                    out=mu_state[:, blocks_from(first_block(r) % STORE_BLOCKS), :],
-                    in0=mu_ps[:, :, 0:STATE],
-                    in1=bmu_f32[:, e : e + 1, 0:STATE].to_broadcast([P, ROUND, STATE]),
+                    out=mu_sb[:, blocks_from(e), :],
+                    in0=live["mu_ps", r][:],
+                    in1=bmu_f32[:, e : e + 1, :].to_broadcast([P, ROUND, OUT]),
                     op=ALU.add,
                 )
-                nc.vector.tensor_tensor(
-                    out=mu_reward[:, blocks_from(first_block(r)), :],
-                    in0=mu_ps[:, :, STATE:OUT],
-                    in1=bmu_f32[:, e : e + 1, STATE:OUT].to_broadcast([P, ROUND, REWARD]),
-                    op=ALU.add,
-                )
-                if r % STORE_ROUNDS == STORE_ROUNDS - 1:
-                    stored = r // STORE_ROUNDS * STORE_BLOCKS
-                    nc.sync.dma_start(out=ds_mu[:, stored : stored + STORE_BLOCKS, :], in_=mu_state[:])
+                if e == MEMBERS - 1:
+                    stored = slice(r // MEMBERS * GROUP, (r // MEMBERS + 1) * GROUP)
+                    nc.sync.dma_start(out=ds_mu[:, stored, :], in_=mu_sb[:, :, 0:STATE])
+                    nc.sync.dma_start(out=r_mu[:, stored, :], in_=mu_sb[:, :, STATE:OUT])
 
             def run(stage, r):
                 if 0 <= r < ROUNDS:
@@ -308,11 +300,9 @@ def tile_ensembleenvprob_pa_t_e_kernel(
                 run(add_bh, i - 1)
                 run(heads, i - 4)
 
-        nc.sync.dma_start(out=r_mu, in_=mu_reward[:])
-
         with tc.psum_pool(name="psum_sg", bufs=4) as psum_sg:
             for first in range(0, BLOCKS, STORE_BLOCKS):
-                sg_state = results.tile([P, STORE_BLOCKS, STATE], F32, tag="staged")
+                sg_state = results.tile([P, STORE_BLOCKS, STATE], F32)
                 for part in range(0, STORE_BLOCKS, SQRT_BLOCKS):
                     blocks = slice(first + part, first + part + SQRT_BLOCKS)
                     sgT = work.tile([P, SQRT_BLOCKS, P], F32)

@@ -20,10 +20,10 @@ OUT = 128
 STATE = 120
 REWARD = OUT - STATE
 BLOCKS = 96
-ROUND = 2
+ROUND = 4
 ROUNDS = BLOCKS // ROUND
 GROUP = ROUND * MEMBERS
-STORE_BLOCKS = 2 * GROUP
+STORE_BLOCKS = GROUP
 SQRT_BLOCKS = 4
 
 FLOPS = 2 * 4096 * MEMBERS * (HID * HID + 2 * HID * OUT)
@@ -83,7 +83,7 @@ def tile_ensembleenvprob_pa_t_e_kernel(
         stack.enter_context(tc.manual_schedule())
         keep = stack.enter_context(tc.tile_pool(name="keep", bufs=1))
         work = stack.enter_context(tc.tile_pool(name="work", bufs=2))
-        results = stack.enter_context(tc.tile_pool(name="results", bufs=3))
+        results = stack.enter_context(tc.tile_pool(name="results", bufs=4))
 
         ident = keep.tile([P, P], F32)
         make_identity(nc, ident[:])
@@ -95,12 +95,18 @@ def tile_ensembleenvprob_pa_t_e_kernel(
         def load_h(c):
             nc.sync.dma_start(out=h_tiles[c][:], in_=h_blocks[:, c * GROUP : (c + 1) * GROUP, :])
 
-        load_h(0)
-        wh_words, wh_planes = load_weight(nc, keep, Wh_words, Wh_scales, HID, "wh")
-        load_h(1)
+        def load_h_member(e):
+            nc.sync.dma_start(
+                out=h_tiles[0][:, e:GROUP:MEMBERS, :], in_=h_blocks[:, e:GROUP:MEMBERS, :]
+            )
+
+        load_h_member(0)
+        wh_raw, wh_raw_planes = load_weight(nc, keep, Wh_words, Wh_scales, HID, "wh_raw")
+        load_h_member(1)
+        load_h_member(2)
         wmu_words, wmu_planes = load_weight(nc, keep, Wmu_words, Wmu_scales, OUT, "wmu")
         wsig_words, wsig_planes = load_weight(nc, keep, Wsig_words, Wsig_scales, OUT, "wsig")
-        for c in range(2, BLOCKS // GROUP):
+        for c in range(1, BLOCKS // GROUP):
             load_h(c)
 
         rows_bf = keep.tile([P, P], BF16)
@@ -110,8 +116,8 @@ def tile_ensembleenvprob_pa_t_e_kernel(
         nc.scalar.dma_start(out=rows_bf[4:5, STATE:OUT], in_=max_lv_r)
         nc.scalar.dma_start(out=rows_bf[5:6, 0:STATE], in_=min_lv_s)
         nc.scalar.dma_start(out=rows_bf[6:7, STATE:OUT], in_=min_lv_r)
-        bh_bf = keep.tile([P, MEMBERS * HID], BF16)
-        nc.scalar.dma_start(out=bh_bf[:], in_=bh.rearrange("e k -> (e k)").partition_broadcast(P))
+        bh_bf = keep.tile([P, MEMBERS, PACK], BF16)
+        nc.scalar.dma_start(out=bh_bf[:], in_=bh.rearrange("e (p t) -> p e t", t=PACK))
         bmu_bf = keep.tile([P, MEMBERS, OUT], BF16)
         nc.scalar.dma_start(
             out=bmu_bf[:].rearrange("n e o -> n (e o)"),
@@ -125,16 +131,25 @@ def tile_ensembleenvprob_pa_t_e_kernel(
             live = {}
 
             def transpose_h(r):
-                hT = psum.tile([P, ROUND, 2, P], F32)
-                for g in range(ROUND):
-                    words = h_tiles[r // MEMBERS][:, r % MEMBERS + MEMBERS * g, :].bitcast(F32)
-                    for u in range(2):
-                        nc.tensor.transpose(out=hT[:, g, u, :], in_=words[:, u : HID // 2 : 2], identity=ident[:])
-                live["hT", r] = hT
+                halves = []
+                for half in range(2):
+                    hT = psum.tile([P, ROUND // 2, 2, P], F32, tag="hT%d" % half)
+                    for g in range(ROUND // 2):
+                        block = r % MEMBERS + MEMBERS * (half * ROUND // 2 + g)
+                        words = h_tiles[r // MEMBERS][:, block, :].bitcast(F32)
+                        for u in range(2):
+                            nc.tensor.transpose(out=hT[:, g, u, :], in_=words[:, u : HID // 2 : 2], identity=ident[:])
+                    halves.append(hT)
+                live["hT", r] = halves
 
             def regroup_h(r):
                 h_grouped = work.tile([P, ROUND, P, PACK], BF16, align_bytes=64)
-                nc.scalar.copy(out=h_grouped[:].bitcast(F32), in_=live["hT", r][:].rearrange("p g u n -> p g n u"))
+                for half, copy in enumerate((nc.scalar.copy, nc.vector.tensor_copy)):
+                    blocks = slice(half * ROUND // 2, (half + 1) * ROUND // 2)
+                    copy(
+                        out=h_grouped[:, blocks].rearrange("p g n t -> p (g n t)").bitcast(F32).rearrange("p (g n u) -> p g n u", g=ROUND // 2, u=2),
+                        in_=live["hT", r][half][:].rearrange("p g u n -> p g n u"),
+                    )
                 live["h_grouped", r] = h_grouped
 
             def quantise_h(r):
@@ -150,45 +165,31 @@ def tile_ensembleenvprob_pa_t_e_kernel(
             def layer_1(r):
                 h_codes, h_scales = live["h_mx", r]
                 e = r % MEMBERS
-                for g in range(ROUND):
-                    x_ps = psum.tile([P, HID], F32, tag="x_ps%d" % g)
+                for t in range(PACK):
+                    x_ps = psum.tile([P, ROUND * P], F32, tag="x_ps%d" % t)
                     nc.tensor.matmul_mx(
                         out=x_ps[:],
-                        lhsT=h_codes[:, g * P : (g + 1) * P].bitcast(FP8X4),
-                        lhsT_scale=h_scales[:, g * P : (g + 1) * P],
-                        rhs=wh_words[:, e, :].bitcast(FP8X4),
-                        rhs_scale=wh_planes[:, e, :],
+                        lhsT=wh_words[:, e, t * P : (t + 1) * P].bitcast(FP8X4),
+                        lhsT_scale=wh_planes[:, e, t * P : (t + 1) * P],
+                        rhs=h_codes[:].bitcast(FP8X4),
+                        rhs_scale=h_scales[:],
                         start=True,
                         stop=True,
                     )
-                    live["x_ps", r, g] = x_ps
-
-            def add_bh(r):
-                x_sb = work.tile([P, ROUND, PACK, P], F32, bufs=3)
-                e = r % MEMBERS
-                for g in range(ROUND):
-                    nc.vector.tensor_tensor(
-                        out=x_sb[:, g],
-                        in0=live["x_ps", r, g][:].rearrange("n (p t) -> n t p", t=PACK),
-                        in1=bh_tp[:, e],
-                        op=ALU.add,
-                    )
-                live["x_sb", r] = x_sb
-
-            def transpose_x(r):
-                x_sb = live["x_sb", r]
-                for g in range(ROUND):
-                    xT = psum.tile([P, PACK, P], F32, tag="xT%d" % g)
-                    for t in range(PACK):
-                        nc.tensor.transpose(out=xT[:, t, :], in_=x_sb[:, g, t, :], identity=ident[:])
-                    live["xT", r, g] = xT
+                    live["x_ps", r, t] = x_ps
 
             def swish(r):
-                g_grouped = work.tile([P, ROUND, P, PACK], BF16, align_bytes=64)
-                for g in range(ROUND):
+                e = r % MEMBERS
+                g_planes = work.tile([P, PACK, ROUND * P], BF16, align_bytes=64)
+                for t in range(PACK):
                     nc.scalar.activation(
-                        out=g_grouped[:, g], in_=live["xT", r, g][:].rearrange("p t n -> p n t"), func=ACT.Silu
+                        out=g_planes[:, t, :], in_=live["x_ps", r, t][:], func=ACT.Silu, bias=bh_cols[:, e, t : t + 1]
                     )
+                live["g_planes", r] = g_planes
+
+            def interleave_g(r):
+                g_grouped = work.tile([P, ROUND * P, PACK], BF16, align_bytes=64)
+                nc.vector.tensor_copy(out=g_grouped[:], in_=live["g_planes", r][:].rearrange("p t n -> p n t"))
                 live["g_grouped", r] = g_grouped
 
             def quantise_g(r):
@@ -197,7 +198,7 @@ def tile_ensembleenvprob_pa_t_e_kernel(
                 nc.vector.quantize_mx(
                     out=g_codes[:].bitcast(FP8X4),
                     scales=g_scales[:],
-                    in_=live["g_grouped", r][:].rearrange("p g n t -> p (g n t)"),
+                    in_=live["g_grouped", r][:].rearrange("p n t -> p (n t)"),
                 )
                 live["g_mx", r] = (g_codes, g_scales)
 
@@ -240,7 +241,7 @@ def tile_ensembleenvprob_pa_t_e_kernel(
             def add_bmu(r):
                 e = r % MEMBERS
                 if e == 0:
-                    mu_group = results.tile([P, GROUP, OUT], F32, bufs=4)
+                    mu_group = results.tile([P, GROUP, OUT], F32, tag="out")
                     live["mu_sb"] = mu_group
                 mu_sb = live["mu_sb"]
                 nc.vector.tensor_tensor(
@@ -262,9 +263,21 @@ def tile_ensembleenvprob_pa_t_e_kernel(
             regroup_h(0)
             quantise_h(0)
 
+            wh_words = keep.tile([P, MEMBERS, HID], I32, align_bytes=64)
+            wh_planes = keep.tile([P, MEMBERS, HID], U8, align_bytes=64)
+            for e in range(MEMBERS):
+                nc.vector.tensor_copy(
+                    out=wh_words[:, e, :].rearrange("p (t m) -> p t m", t=PACK),
+                    in_=wh_raw[:, e, :].bitcast(I32).rearrange("p (m t) -> p t m", t=PACK),
+                )
+                nc.vector.tensor_copy(
+                    out=wh_planes[:, e, :].rearrange("p (t m) -> p t m", t=PACK),
+                    in_=wh_raw_planes[:, e, :].rearrange("p (m t) -> p t m", t=PACK),
+                )
+
             rows_f32 = keep.tile([P, P], F32)
             nc.vector.tensor_copy(out=rows_f32[:], in_=rows_bf[:])
-            cols_ps = psum.tile([P, P], F32)
+            cols_ps = psum.tile([P, P], F32, tag="mu_ps")
             nc.tensor.transpose(out=cols_ps[:], in_=rows_f32[:], identity=ident[:])
             cols = keep.tile([P, 8], F32)
             nc.vector.tensor_copy(out=cols[:], in_=cols_ps[:, 0:8])
@@ -282,30 +295,29 @@ def tile_ensembleenvprob_pa_t_e_kernel(
             nc.vector.tensor_scalar(
                 out=tanh_bias[:], in0=cols[:, 0:MEMBERS], scalar1=half_hi[:, 0:1], scalar2=None, op0=ALU.subtract
             )
-            bh_tp = keep.tile([P, MEMBERS, PACK, P], F32)
-            nc.vector.tensor_copy(out=bh_tp[:], in_=bh_bf[:].rearrange("n (e p t) -> n e t p", e=MEMBERS, t=PACK))
+            bh_cols = keep.tile([P, MEMBERS, PACK], F32)
+            nc.vector.tensor_copy(out=bh_cols[:], in_=bh_bf[:])
             bmu_f32 = keep.tile([P, MEMBERS, OUT], F32)
             nc.vector.tensor_copy(out=bmu_f32[:], in_=bmu_bf[:])
 
-            for i in range(1, ROUNDS + 6):
-                run(tanh_sigma, i - 5)
-                run(quantise_g, i - 4)
-                run(add_bmu, i - 5)
+            for i in range(1, ROUNDS + 4):
+                run(add_bmu, i - 4)
+                run(tanh_sigma, i - 4)
                 run(transpose_h, i)
                 run(regroup_h, i)
+                run(interleave_g, i - 2)
                 run(quantise_h, i)
-                run(transpose_x, i - 3)
-                run(swish, i - 3)
+                run(quantise_g, i - 2)
                 run(layer_1, i - 1)
-                run(add_bh, i - 1)
-                run(heads, i - 4)
+                run(swish, i - 1)
+                run(heads, i - 3)
 
         with tc.psum_pool(name="psum_sg", bufs=4) as psum_sg:
             for first in range(0, BLOCKS, STORE_BLOCKS):
-                sg_state = results.tile([P, STORE_BLOCKS, STATE], F32)
+                sg_state = results.tile([P, STORE_BLOCKS, STATE], F32, tag="out")
                 for part in range(0, STORE_BLOCKS, SQRT_BLOCKS):
                     blocks = slice(first + part, first + part + SQRT_BLOCKS)
-                    sgT = work.tile([P, SQRT_BLOCKS, P], F32)
+                    sgT = work.tile([P, SQRT_BLOCKS, P], F32, bufs=3)
                     nc.scalar.activation(
                         out=sgT[:],
                         in_=tanh_all[:, blocks, :],

@@ -23,14 +23,13 @@ BLOCKS = 96
 ROUND = 4
 ROUNDS = BLOCKS // ROUND
 GROUP = ROUND * MEMBERS
-STORE_BLOCKS = GROUP
+REWARD_BLOCKS = 24
 SQRT_BLOCKS = 4
 
 FLOPS = 2 * 4096 * MEMBERS * (HID * HID + 2 * HID * OUT)
 
 
-def load_weight(nc, pool, words_dram, scales_dram, width, label):
-    words = pool.tile([P, MEMBERS, PACK * width], U8, name=label + "_words", align_bytes=64)
+def load_scales(nc, pool, scales_dram, width, label):
     planes = pool.tile([P, MEMBERS, width], U8, name=label + "_planes", align_bytes=64)
     nc.vector.memset(planes[:].bitcast(I32), 0)
     for quadrant in range(4):
@@ -38,11 +37,14 @@ def load_weight(nc, pool, words_dram, scales_dram, width, label):
             out=planes[32 * quadrant : 32 * quadrant + 4].bitcast(I32),
             in_=scales_dram[:, 4 * quadrant : 4 * quadrant + 4, :].rearrange("e r n -> r e n").bitcast(I32),
         )
+    return planes
+
+
+def load_words(nc, words, words_dram, members):
     nc.sync.dma_start(
-        out=words[:].bitcast(I32),
-        in_=words_dram.rearrange("e p n t -> p e (n t)").bitcast(I32),
+        out=words[:, members, :].bitcast(I32),
+        in_=words_dram[members].rearrange("e p n t -> p e (n t)").bitcast(I32),
     )
-    return words, planes
 
 
 def tile_ensembleenvprob_pa_t_e_kernel(
@@ -83,32 +85,45 @@ def tile_ensembleenvprob_pa_t_e_kernel(
         stack.enter_context(tc.manual_schedule())
         keep = stack.enter_context(tc.tile_pool(name="keep", bufs=1))
         work = stack.enter_context(tc.tile_pool(name="work", bufs=2))
-        results = stack.enter_context(tc.tile_pool(name="results", bufs=4))
+        results = stack.enter_context(tc.tile_pool(name="results", bufs=3))
 
         ident = keep.tile([P, P], F32)
         make_identity(nc, ident[:])
 
         h_tiles = []
-        for c in range(BLOCKS // GROUP):
-            h_tiles.append(keep.tile([P, GROUP, HID], BF16, name="h%d" % c))
+        for r in range(ROUNDS):
+            h_tiles.append(keep.tile([P, ROUND, HID], BF16, name="h%d" % r))
 
-        def load_h(c):
-            nc.sync.dma_start(out=h_tiles[c][:], in_=h_blocks[:, c * GROUP : (c + 1) * GROUP, :])
+        def load_h(r, blocks=slice(0, ROUND)):
+            first = first_block(r) + MEMBERS * blocks.start
+            last = first_block(r) + MEMBERS * (blocks.stop - 1)
+            nc.sync.dma_start(out=h_tiles[r][:, blocks, :], in_=h_blocks[:, first : last + 1 : MEMBERS, :])
 
-        def load_h_member(e):
-            nc.sync.dma_start(
-                out=h_tiles[0][:, e:GROUP:MEMBERS, :], in_=h_blocks[:, e:GROUP:MEMBERS, :]
-            )
+        wh_raw = keep.tile([P, MEMBERS, PACK * HID], U8, align_bytes=64)
+        wmu_words = keep.tile([P, MEMBERS, PACK * OUT], U8, align_bytes=64)
+        wsig_words = keep.tile([P, MEMBERS, PACK * OUT], U8, align_bytes=64)
+        everyone = slice(0, MEMBERS)
 
-        load_h_member(0)
-        wh_raw, wh_raw_planes = load_weight(nc, keep, Wh_words, Wh_scales, HID, "wh_raw")
-        load_h_member(1)
-        load_h_member(2)
-        wmu_words, wmu_planes = load_weight(nc, keep, Wmu_words, Wmu_scales, OUT, "wmu")
-        wsig_words, wsig_planes = load_weight(nc, keep, Wsig_words, Wsig_scales, OUT, "wsig")
-        for c in range(1, BLOCKS // GROUP):
-            load_h(c)
+        wh_raw_planes = load_scales(nc, keep, Wh_scales, HID, "wh_raw")
+        load_h(0, slice(0, ROUND // 2))
+        load_words(nc, wh_raw, Wh_words, slice(0, 1))
+        load_h(0, slice(ROUND // 2, ROUND))
+        load_h(1)
+        load_words(nc, wh_raw, Wh_words, slice(1, 2))
+        load_h(2)
+        load_words(nc, wh_raw, Wh_words, slice(2, 3))
+        wmu_planes = load_scales(nc, keep, Wmu_scales, OUT, "wmu")
+        wsig_planes = load_scales(nc, keep, Wsig_scales, OUT, "wsig")
+        load_words(nc, wmu_words, Wmu_words, everyone)
+        load_words(nc, wsig_words, Wsig_words, everyone)
+        for r in range(MEMBERS, ROUNDS):
+            load_h(r)
 
+        bh_bf = keep.tile([P, MEMBERS, PACK], BF16)
+        nc.scalar.dma_start(out=bh_bf[:], in_=bh.rearrange("e (p t) -> p e t", t=PACK))
+        idle = keep.tile([P, 1], F32)
+        nc.vector.memset(idle[:], 0.0)
+        nc.scalar.activation(out=idle[:], in_=idle[:], func=ACT.Silu)
         rows_bf = keep.tile([P, P], BF16)
         nc.vector.memset(rows_bf[:], 0.0)
         nc.scalar.dma_start(out=rows_bf[0:MEMBERS, :], in_=bsig)
@@ -116,8 +131,6 @@ def tile_ensembleenvprob_pa_t_e_kernel(
         nc.scalar.dma_start(out=rows_bf[4:5, STATE:OUT], in_=max_lv_r)
         nc.scalar.dma_start(out=rows_bf[5:6, 0:STATE], in_=min_lv_s)
         nc.scalar.dma_start(out=rows_bf[6:7, STATE:OUT], in_=min_lv_r)
-        bh_bf = keep.tile([P, MEMBERS, PACK], BF16)
-        nc.scalar.dma_start(out=bh_bf[:], in_=bh.rearrange("e (p t) -> p e t", t=PACK))
         bmu_bf = keep.tile([P, MEMBERS, OUT], BF16)
         nc.scalar.dma_start(
             out=bmu_bf[:].rearrange("n e o -> n (e o)"),
@@ -135,8 +148,7 @@ def tile_ensembleenvprob_pa_t_e_kernel(
                 for half in range(2):
                     hT = psum.tile([P, ROUND // 2, 2, P], F32, tag="hT%d" % half)
                     for g in range(ROUND // 2):
-                        block = r % MEMBERS + MEMBERS * (half * ROUND // 2 + g)
-                        words = h_tiles[r // MEMBERS][:, block, :].bitcast(F32)
+                        words = h_tiles[r][:, half * ROUND // 2 + g, :].bitcast(F32)
                         for u in range(2):
                             nc.tensor.transpose(out=hT[:, g, u, :], in_=words[:, u : HID // 2 : 2], identity=ident[:])
                     halves.append(hT)
@@ -144,7 +156,8 @@ def tile_ensembleenvprob_pa_t_e_kernel(
 
             def regroup_h(r):
                 h_grouped = work.tile([P, ROUND, P, PACK], BF16, align_bytes=64)
-                for half, copy in enumerate((nc.scalar.copy, nc.vector.tensor_copy)):
+                second = nc.scalar.copy if r % 3 == 0 else nc.vector.tensor_copy
+                for half, copy in enumerate((nc.scalar.copy, second)):
                     blocks = slice(half * ROUND // 2, (half + 1) * ROUND // 2)
                     copy(
                         out=h_grouped[:, blocks].rearrange("p g n t -> p (g n t)").bitcast(F32).rearrange("p (g n u) -> p g n u", g=ROUND // 2, u=2),
@@ -205,6 +218,16 @@ def tile_ensembleenvprob_pa_t_e_kernel(
             def heads(r):
                 g_codes, g_scales = live["g_mx", r]
                 e = r % MEMBERS
+                sigT_ps = psum.tile([P, ROUND, P], F32)
+                nc.tensor.matmul_mx(
+                    out=sigT_ps[:].rearrange("o g n -> o (g n)"),
+                    lhsT=wsig_words[:, e, :].bitcast(FP8X4),
+                    lhsT_scale=wsig_planes[:, e, :],
+                    rhs=g_codes[:].bitcast(FP8X4),
+                    rhs_scale=g_scales[:],
+                    start=True,
+                    stop=True,
+                )
                 mu_ps = psum.tile([P, ROUND, OUT], F32)
                 for g in range(ROUND):
                     nc.tensor.matmul_mx(
@@ -216,16 +239,6 @@ def tile_ensembleenvprob_pa_t_e_kernel(
                         start=True,
                         stop=True,
                     )
-                sigT_ps = psum.tile([P, ROUND, P], F32)
-                nc.tensor.matmul_mx(
-                    out=sigT_ps[:].rearrange("o g n -> o (g n)"),
-                    lhsT=wsig_words[:, e, :].bitcast(FP8X4),
-                    lhsT_scale=wsig_planes[:, e, :],
-                    rhs=g_codes[:].bitcast(FP8X4),
-                    rhs_scale=g_scales[:],
-                    start=True,
-                    stop=True,
-                )
                 live["mu_ps", r] = mu_ps
                 live["sigT_ps", r] = sigT_ps
 
@@ -241,7 +254,7 @@ def tile_ensembleenvprob_pa_t_e_kernel(
             def add_bmu(r):
                 e = r % MEMBERS
                 if e == 0:
-                    mu_group = results.tile([P, GROUP, OUT], F32, tag="out")
+                    mu_group = results.tile([P, GROUP, OUT], F32)
                     live["mu_sb"] = mu_group
                 mu_sb = live["mu_sb"]
                 nc.vector.tensor_tensor(
@@ -259,48 +272,46 @@ def tile_ensembleenvprob_pa_t_e_kernel(
                 if 0 <= r < ROUNDS:
                     stage(r)
 
-            transpose_h(0)
-            regroup_h(0)
-            quantise_h(0)
-
             wh_words = keep.tile([P, MEMBERS, HID], I32, align_bytes=64)
             wh_planes = keep.tile([P, MEMBERS, HID], U8, align_bytes=64)
-            for e in range(MEMBERS):
-                nc.vector.tensor_copy(
-                    out=wh_words[:, e, :].rearrange("p (t m) -> p t m", t=PACK),
-                    in_=wh_raw[:, e, :].bitcast(I32).rearrange("p (m t) -> p t m", t=PACK),
-                )
+
+            def regroup_wh(e):
                 nc.vector.tensor_copy(
                     out=wh_planes[:, e, :].rearrange("p (t m) -> p t m", t=PACK),
                     in_=wh_raw_planes[:, e, :].rearrange("p (m t) -> p t m", t=PACK),
                 )
+                nc.vector.tensor_copy(
+                    out=wh_words[:, e, :].rearrange("p (t m) -> p t m", t=PACK),
+                    in_=wh_raw[:, e, :].bitcast(I32).rearrange("p (m t) -> p t m", t=PACK),
+                )
 
-            rows_f32 = keep.tile([P, P], F32)
-            nc.vector.tensor_copy(out=rows_f32[:], in_=rows_bf[:])
-            cols_ps = psum.tile([P, P], F32, tag="mu_ps")
-            nc.tensor.transpose(out=cols_ps[:], in_=rows_f32[:], identity=ident[:])
-            cols = keep.tile([P, 8], F32)
-            nc.vector.tensor_copy(out=cols[:], in_=cols_ps[:, 0:8])
-            hi_lo = keep.tile([P, 2], F32)
-            nc.vector.tensor_tensor(out=hi_lo[:], in0=cols[:, 3:6:2], in1=cols[:, 4:7:2], op=ALU.add)
-            exp_hi_lo = keep.tile([P, 2], F32)
-            nc.scalar.activation(out=exp_hi_lo[:], in_=hi_lo[:], func=ACT.Exp)
-            sqrt_scale = keep.tile([P, 1], F32)
-            nc.vector.tensor_scalar(out=sqrt_scale[:], in0=exp_hi_lo[:, 0:1], scalar1=0.5, scalar2=None, op0=ALU.mult)
-            sqrt_bias = keep.tile([P, 1], F32)
-            nc.vector.tensor_tensor(out=sqrt_bias[:], in0=sqrt_scale[:], in1=exp_hi_lo[:, 1:2], op=ALU.add)
-            half_hi = keep.tile([P, 1], F32)
-            nc.vector.tensor_scalar(out=half_hi[:], in0=hi_lo[:, 0:1], scalar1=0.5, scalar2=None, op0=ALU.mult)
-            tanh_bias = keep.tile([P, MEMBERS], F32)
-            nc.vector.tensor_scalar(
-                out=tanh_bias[:], in0=cols[:, 0:MEMBERS], scalar1=half_hi[:, 0:1], scalar2=None, op0=ALU.subtract
-            )
             bh_cols = keep.tile([P, MEMBERS, PACK], F32)
-            nc.vector.tensor_copy(out=bh_cols[:], in_=bh_bf[:])
             bmu_f32 = keep.tile([P, MEMBERS, OUT], F32)
-            nc.vector.tensor_copy(out=bmu_f32[:], in_=bmu_bf[:])
+            tanh_bias = keep.tile([P, MEMBERS], F32)
+            hi_lo = keep.tile([P, 2], F32)
+            sqrt_scale = keep.tile([P, 1], F32)
+            sqrt_bias = keep.tile([P, 1], F32)
 
-            for i in range(1, ROUNDS + 4):
+            def prepare_heads():
+                nc.vector.tensor_copy(out=bmu_f32[:], in_=bmu_bf[:])
+                rows_f32 = keep.tile([P, P], F32)
+                nc.vector.tensor_copy(out=rows_f32[:], in_=rows_bf[:])
+                cols_ps = psum.tile([P, P], F32, tag="mu_ps")
+                nc.tensor.transpose(out=cols_ps[:], in_=rows_f32[:], identity=ident[:])
+                cols = keep.tile([P, 8], F32)
+                nc.vector.tensor_copy(out=cols[:], in_=cols_ps[:, 0:8])
+                nc.vector.tensor_tensor(out=hi_lo[:], in0=cols[:, 3:6:2], in1=cols[:, 4:7:2], op=ALU.add)
+                half_hi = keep.tile([P, 1], F32)
+                nc.vector.tensor_scalar(out=half_hi[:], in0=hi_lo[:, 0:1], scalar1=0.5, scalar2=None, op0=ALU.mult)
+                nc.vector.tensor_scalar(
+                    out=tanh_bias[:], in0=cols[:, 0:MEMBERS], scalar1=half_hi[:, 0:1], scalar2=None, op0=ALU.subtract
+                )
+
+            exp_hi_lo = keep.tile([P, 2], F32)
+
+            regroup_wh(0)
+            nc.vector.tensor_copy(out=bh_cols[:], in_=bh_bf[:])
+            for i in range(ROUNDS + 4):
                 run(add_bmu, i - 4)
                 run(tanh_sigma, i - 4)
                 run(transpose_h, i)
@@ -311,24 +322,33 @@ def tile_ensembleenvprob_pa_t_e_kernel(
                 run(layer_1, i - 1)
                 run(swish, i - 1)
                 run(heads, i - 3)
+                if i in (0, 1):
+                    regroup_wh(i + 1)
+                if i == 1:
+                    prepare_heads()
+                if i == ROUNDS:
+                    nc.scalar.activation(out=exp_hi_lo[:], in_=hi_lo[:], func=ACT.Exp)
+            nc.vector.tensor_scalar(out=sqrt_scale[:], in0=exp_hi_lo[:, 0:1], scalar1=0.5, scalar2=None, op0=ALU.mult)
+            nc.vector.tensor_tensor(out=sqrt_bias[:], in0=sqrt_scale[:], in1=exp_hi_lo[:, 1:2], op=ALU.add)
 
         with tc.psum_pool(name="psum_sg", bufs=4) as psum_sg:
-            for first in range(0, BLOCKS, STORE_BLOCKS):
-                sg_state = results.tile([P, STORE_BLOCKS, STATE], F32, tag="out")
-                for part in range(0, STORE_BLOCKS, SQRT_BLOCKS):
-                    blocks = slice(first + part, first + part + SQRT_BLOCKS)
-                    sgT = work.tile([P, SQRT_BLOCKS, P], F32, bufs=3)
-                    nc.scalar.activation(
-                        out=sgT[:],
-                        in_=tanh_all[:, blocks, :],
-                        func=ACT.Sqrt,
-                        bias=sqrt_bias[:, 0:1],
-                        scale=sqrt_scale[:, 0:1],
-                    )
-                    sg_ps = psum_sg.tile([P, SQRT_BLOCKS, OUT], F32)
-                    for g in range(SQRT_BLOCKS):
-                        nc.tensor.transpose(out=sg_ps[:, g, :], in_=sgT[:, g, :], identity=ident[:])
-                    nc.vector.tensor_copy(out=sg_state[:, part : part + SQRT_BLOCKS, :], in_=sg_ps[:, :, 0:STATE])
-                    nc.vector.tensor_copy(out=sg_reward[:, blocks, :], in_=sg_ps[:, :, STATE:OUT])
-                nc.sync.dma_start(out=ds_sg[:, first : first + STORE_BLOCKS, :], in_=sg_state[:])
-            nc.sync.dma_start(out=r_sg, in_=sg_reward[:])
+            for first in range(0, BLOCKS, SQRT_BLOCKS):
+                blocks = slice(first, first + SQRT_BLOCKS)
+                sgT = work.tile([P, SQRT_BLOCKS, P], F32, bufs=3)
+                nc.scalar.activation(
+                    out=sgT[:],
+                    in_=tanh_all[:, blocks, :],
+                    func=ACT.Sqrt,
+                    bias=sqrt_bias[:, 0:1],
+                    scale=sqrt_scale[:, 0:1],
+                )
+                sg_ps = psum_sg.tile([P, SQRT_BLOCKS, OUT], F32)
+                for g in range(SQRT_BLOCKS):
+                    nc.tensor.transpose(out=sg_ps[:, g, :], in_=sgT[:, g, :], identity=ident[:])
+                sg_state = results.tile([P, SQRT_BLOCKS, STATE], F32, bufs=4)
+                nc.vector.tensor_copy(out=sg_state[:], in_=sg_ps[:, :, 0:STATE])
+                nc.vector.tensor_copy(out=sg_reward[:, blocks, :], in_=sg_ps[:, :, STATE:OUT])
+                nc.sync.dma_start(out=ds_sg[:, blocks, :], in_=sg_state[:])
+                if blocks.stop % REWARD_BLOCKS == 0:
+                    stored = slice(blocks.stop - REWARD_BLOCKS, blocks.stop)
+                    nc.sync.dma_start(out=r_sg[:, stored, :], in_=sg_reward[:, stored, :])

@@ -22,6 +22,7 @@ REWARD = OUT - STATE
 BLOCKS = 96
 ROUND = 4
 ROUNDS = BLOCKS // ROUND
+AHEAD = 8
 GROUP = ROUND * MEMBERS
 REWARD_BLOCKS = 24
 SQRT_BLOCKS = 4
@@ -86,18 +87,25 @@ def tile_ensembleenvprob_pa_t_e_kernel(
         keep = stack.enter_context(tc.tile_pool(name="keep", bufs=1))
         work = stack.enter_context(tc.tile_pool(name="work", bufs=2))
         results = stack.enter_context(tc.tile_pool(name="results", bufs=3))
+        loads = stack.enter_context(tc.tile_pool(name="loads", bufs=AHEAD))
 
+        rows_bf = keep.tile([P, P], BF16)
+        nc.vector.memset(rows_bf[:], 0.0)
         ident = keep.tile([P, P], F32)
         make_identity(nc, ident[:])
 
-        h_tiles = []
-        for r in range(ROUNDS):
-            h_tiles.append(keep.tile([P, ROUND, HID], BF16, name="h%d" % r))
+        h_tiles = {}
 
-        def load_h(r, blocks=slice(0, ROUND)):
-            first = first_block(r) + MEMBERS * blocks.start
-            last = first_block(r) + MEMBERS * (blocks.stop - 1)
-            nc.sync.dma_start(out=h_tiles[r][:, blocks, :], in_=h_blocks[:, first : last + 1 : MEMBERS, :])
+        def load_h(r, parts=1):
+            h_tile = loads.tile([P, ROUND, HID], BF16)
+            for part in range(parts):
+                first = part * ROUND // parts
+                last = (part + 1) * ROUND // parts - 1
+                nc.sync.dma_start(
+                    out=h_tile[:, first : last + 1, :],
+                    in_=h_blocks[:, first_block(r) + MEMBERS * first : first_block(r) + MEMBERS * last + 1 : MEMBERS, :],
+                )
+            h_tiles[r] = h_tile
 
         wh_raw = keep.tile([P, MEMBERS, PACK * HID], U8, align_bytes=64)
         wmu_words = keep.tile([P, MEMBERS, PACK * OUT], U8, align_bytes=64)
@@ -105,9 +113,13 @@ def tile_ensembleenvprob_pa_t_e_kernel(
         everyone = slice(0, MEMBERS)
 
         wh_raw_planes = load_scales(nc, keep, Wh_scales, HID, "wh_raw")
-        load_h(0, slice(0, ROUND // 2))
+        load_h(0, parts=2)
         load_words(nc, wh_raw, Wh_words, slice(0, 1))
-        load_h(0, slice(ROUND // 2, ROUND))
+        nc.sync.dma_start(out=rows_bf[0:MEMBERS, :], in_=bsig)
+        nc.sync.dma_start(out=rows_bf[3:4, 0:STATE], in_=max_lv_s)
+        nc.sync.dma_start(out=rows_bf[4:5, STATE:OUT], in_=max_lv_r)
+        nc.sync.dma_start(out=rows_bf[5:6, 0:STATE], in_=min_lv_s)
+        nc.sync.dma_start(out=rows_bf[6:7, STATE:OUT], in_=min_lv_r)
         load_h(1)
         load_words(nc, wh_raw, Wh_words, slice(1, 2))
         load_h(2)
@@ -116,26 +128,19 @@ def tile_ensembleenvprob_pa_t_e_kernel(
         wsig_planes = load_scales(nc, keep, Wsig_scales, OUT, "wsig")
         load_words(nc, wmu_words, Wmu_words, everyone)
         load_words(nc, wsig_words, Wsig_words, everyone)
-        for r in range(MEMBERS, ROUNDS):
+        for r in range(MEMBERS, AHEAD):
             load_h(r)
 
         bh_bf = keep.tile([P, MEMBERS, PACK], BF16)
         nc.scalar.dma_start(out=bh_bf[:], in_=bh.rearrange("e (p t) -> p e t", t=PACK))
-        idle = keep.tile([P, 1], F32)
-        nc.vector.memset(idle[:], 0.0)
-        nc.scalar.activation(out=idle[:], in_=idle[:], func=ACT.Silu)
-        rows_bf = keep.tile([P, P], BF16)
-        nc.vector.memset(rows_bf[:], 0.0)
-        nc.scalar.dma_start(out=rows_bf[0:MEMBERS, :], in_=bsig)
-        nc.scalar.dma_start(out=rows_bf[3:4, 0:STATE], in_=max_lv_s)
-        nc.scalar.dma_start(out=rows_bf[4:5, STATE:OUT], in_=max_lv_r)
-        nc.scalar.dma_start(out=rows_bf[5:6, 0:STATE], in_=min_lv_s)
-        nc.scalar.dma_start(out=rows_bf[6:7, STATE:OUT], in_=min_lv_r)
         bmu_bf = keep.tile([P, MEMBERS, OUT], BF16)
         nc.scalar.dma_start(
             out=bmu_bf[:].rearrange("n e o -> n (e o)"),
             in_=bmu.rearrange("e o -> (e o)").partition_broadcast(P),
         )
+        idle = keep.tile([P, 1], F32)
+        nc.vector.memset(idle[:], 0.0)
+        nc.scalar.activation(out=idle[:], in_=idle[:], func=ACT.Exp)
 
         tanh_all = keep.tile([P, BLOCKS, P], F32)
         sg_reward = keep.tile([P, BLOCKS, REWARD], F32)
@@ -288,48 +293,56 @@ def tile_ensembleenvprob_pa_t_e_kernel(
             bh_cols = keep.tile([P, MEMBERS, PACK], F32)
             bmu_f32 = keep.tile([P, MEMBERS, OUT], F32)
             tanh_bias = keep.tile([P, MEMBERS], F32)
-            hi_lo = keep.tile([P, 2], F32)
             sqrt_scale = keep.tile([P, 1], F32)
             sqrt_bias = keep.tile([P, 1], F32)
 
-            def prepare_heads():
-                nc.vector.tensor_copy(out=bmu_f32[:], in_=bmu_bf[:])
+            def prepare_constants():
                 rows_f32 = keep.tile([P, P], F32)
                 nc.vector.tensor_copy(out=rows_f32[:], in_=rows_bf[:])
                 cols_ps = psum.tile([P, P], F32, tag="mu_ps")
                 nc.tensor.transpose(out=cols_ps[:], in_=rows_f32[:], identity=ident[:])
                 cols = keep.tile([P, 8], F32)
                 nc.vector.tensor_copy(out=cols[:], in_=cols_ps[:, 0:8])
+                hi_lo = keep.tile([P, 2], F32)
                 nc.vector.tensor_tensor(out=hi_lo[:], in0=cols[:, 3:6:2], in1=cols[:, 4:7:2], op=ALU.add)
+                exp_hi_lo = keep.tile([P, 2], F32)
+                nc.scalar.activation(out=exp_hi_lo[:], in_=hi_lo[:], func=ACT.Exp)
+                live["constants"] = (cols, hi_lo, exp_hi_lo)
+
+            def finish_constants():
+                cols, hi_lo, exp_hi_lo = live["constants"]
                 half_hi = keep.tile([P, 1], F32)
                 nc.vector.tensor_scalar(out=half_hi[:], in0=hi_lo[:, 0:1], scalar1=0.5, scalar2=None, op0=ALU.mult)
                 nc.vector.tensor_scalar(
                     out=tanh_bias[:], in0=cols[:, 0:MEMBERS], scalar1=half_hi[:, 0:1], scalar2=None, op0=ALU.subtract
                 )
+                nc.vector.tensor_scalar(
+                    out=sqrt_scale[:], in0=exp_hi_lo[:, 0:1], scalar1=0.5, scalar2=None, op0=ALU.mult
+                )
+                nc.vector.tensor_tensor(out=sqrt_bias[:], in0=sqrt_scale[:], in1=exp_hi_lo[:, 1:2], op=ALU.add)
+                nc.vector.tensor_copy(out=bmu_f32[:], in_=bmu_bf[:])
 
-            exp_hi_lo = keep.tile([P, 2], F32)
-
-            regroup_wh(0)
             nc.vector.tensor_copy(out=bh_cols[:], in_=bh_bf[:])
+            regroup_wh(0)
             for i in range(ROUNDS + 4):
                 run(add_bmu, i - 4)
                 run(tanh_sigma, i - 4)
                 run(transpose_h, i)
                 run(regroup_h, i)
+                if i == 0:
+                    prepare_constants()
                 run(interleave_g, i - 2)
                 run(quantise_h, i)
                 run(quantise_g, i - 2)
                 run(layer_1, i - 1)
                 run(swish, i - 1)
                 run(heads, i - 3)
+                if i + AHEAD < ROUNDS:
+                    load_h(i + AHEAD)
                 if i in (0, 1):
                     regroup_wh(i + 1)
                 if i == 1:
-                    prepare_heads()
-                if i == ROUNDS:
-                    nc.scalar.activation(out=exp_hi_lo[:], in_=hi_lo[:], func=ACT.Exp)
-            nc.vector.tensor_scalar(out=sqrt_scale[:], in0=exp_hi_lo[:, 0:1], scalar1=0.5, scalar2=None, op0=ALU.mult)
-            nc.vector.tensor_tensor(out=sqrt_bias[:], in0=sqrt_scale[:], in1=exp_hi_lo[:, 1:2], op=ALU.add)
+                    finish_constants()
 
         with tc.psum_pool(name="psum_sg", bufs=4) as psum_sg:
             for first in range(0, BLOCKS, SQRT_BLOCKS):
@@ -345,7 +358,7 @@ def tile_ensembleenvprob_pa_t_e_kernel(
                 sg_ps = psum_sg.tile([P, SQRT_BLOCKS, OUT], F32)
                 for g in range(SQRT_BLOCKS):
                     nc.tensor.transpose(out=sg_ps[:, g, :], in_=sgT[:, g, :], identity=ident[:])
-                sg_state = results.tile([P, SQRT_BLOCKS, STATE], F32, bufs=4)
+                sg_state = results.tile([P, SQRT_BLOCKS, STATE], F32, bufs=8)
                 nc.vector.tensor_copy(out=sg_state[:], in_=sg_ps[:, :, 0:STATE])
                 nc.vector.tensor_copy(out=sg_reward[:, blocks, :], in_=sg_ps[:, :, STATE:OUT])
                 nc.sync.dma_start(out=ds_sg[:, blocks, :], in_=sg_state[:])

@@ -1,3 +1,4 @@
+import math
 from contextlib import ExitStack
 
 import concourse.mybir as mybir
@@ -22,10 +23,14 @@ REWARD = OUT - STATE
 BLOCKS = 96
 ROUND = 4
 ROUNDS = BLOCKS // ROUND
+G_LAG = 3
+SCALAR_LAST = 5
+RUN = 4
 AHEAD = 8
 GROUP = ROUND * MEMBERS
 REWARD_BLOCKS = 24
 SQRT_BLOCKS = 4
+STORE_BLOCKS = 8
 
 FLOPS = 2 * 4096 * MEMBERS * (HID * HID + 2 * HID * OUT)
 
@@ -85,7 +90,7 @@ def tile_ensembleenvprob_pa_t_e_kernel(
     with ExitStack() as stack:
         stack.enter_context(tc.manual_schedule())
         keep = stack.enter_context(tc.tile_pool(name="keep", bufs=1))
-        work = stack.enter_context(tc.tile_pool(name="work", bufs=2))
+        work = stack.enter_context(tc.tile_pool(name="work", bufs=3))
         results = stack.enter_context(tc.tile_pool(name="results", bufs=3))
         loads = stack.enter_context(tc.tile_pool(name="loads", bufs=AHEAD))
 
@@ -112,18 +117,18 @@ def tile_ensembleenvprob_pa_t_e_kernel(
         wsig_words = keep.tile([P, MEMBERS, PACK * OUT], U8, align_bytes=64)
         everyone = slice(0, MEMBERS)
 
-        wh_raw_planes = load_scales(nc, keep, Wh_scales, HID, "wh_raw")
         load_h(0, parts=2)
         load_words(nc, wh_raw, Wh_words, slice(0, 1))
+        wh_raw_planes = load_scales(nc, keep, Wh_scales, HID, "wh_raw")
+        load_h(1)
+        load_words(nc, wh_raw, Wh_words, slice(1, 2))
+        load_h(2)
+        load_words(nc, wh_raw, Wh_words, slice(2, 3))
         nc.sync.dma_start(out=rows_bf[0:MEMBERS, :], in_=bsig)
         nc.sync.dma_start(out=rows_bf[3:4, 0:STATE], in_=max_lv_s)
         nc.sync.dma_start(out=rows_bf[4:5, STATE:OUT], in_=max_lv_r)
         nc.sync.dma_start(out=rows_bf[5:6, 0:STATE], in_=min_lv_s)
         nc.sync.dma_start(out=rows_bf[6:7, STATE:OUT], in_=min_lv_r)
-        load_h(1)
-        load_words(nc, wh_raw, Wh_words, slice(1, 2))
-        load_h(2)
-        load_words(nc, wh_raw, Wh_words, slice(2, 3))
         wmu_planes = load_scales(nc, keep, Wmu_scales, OUT, "wmu")
         wsig_planes = load_scales(nc, keep, Wsig_scales, OUT, "wsig")
         load_words(nc, wmu_words, Wmu_words, everyone)
@@ -140,7 +145,7 @@ def tile_ensembleenvprob_pa_t_e_kernel(
         )
         idle = keep.tile([P, 1], F32)
         nc.vector.memset(idle[:], 0.0)
-        nc.scalar.activation(out=idle[:], in_=idle[:], func=ACT.Exp)
+        nc.scalar.activation(out=idle[:], in_=idle[:], func=ACT.Silu)
 
         tanh_all = keep.tile([P, BLOCKS, P], F32)
         sg_reward = keep.tile([P, BLOCKS, REWARD], F32)
@@ -160,25 +165,31 @@ def tile_ensembleenvprob_pa_t_e_kernel(
                 live["hT", r] = halves
 
             def regroup_h(r):
-                h_grouped = work.tile([P, ROUND, P, PACK], BF16, align_bytes=64)
-                second = nc.scalar.copy if r % 3 == 0 else nc.vector.tensor_copy
+                h_grouped = live["to_quantise", r][:, 0, :].rearrange("p (g n t) -> p g n t", g=ROUND, t=PACK)
+                second = nc.scalar.copy if r == 0 or r >= ROUNDS - SCALAR_LAST else nc.vector.tensor_copy
                 for half, copy in enumerate((nc.scalar.copy, second)):
                     blocks = slice(half * ROUND // 2, (half + 1) * ROUND // 2)
                     copy(
                         out=h_grouped[:, blocks].rearrange("p g n t -> p (g n t)").bitcast(F32).rearrange("p (g n u) -> p g n u", g=ROUND // 2, u=2),
                         in_=live["hT", r][half][:].rearrange("p g u n -> p g n u"),
                     )
-                live["h_grouped", r] = h_grouped
 
-            def quantise_h(r):
-                h_codes = work.tile([P, ROUND * P], U32, align_bytes=64)
-                h_scales = work.tile([P, ROUND * P], U8, align_bytes=64)
+            def new_step(i):
+                to_quantise = work.tile([P, 2, ROUND * P * PACK], BF16, align_bytes=64)
+                live["to_quantise", i] = to_quantise
+
+            def quantise(i):
+                first = 0 if i < ROUNDS else 1
+                last = 1 if i >= G_LAG else 0
+                codes = work.tile([P, 2, ROUND * P], U32, align_bytes=64)
+                scales = work.tile([P, 2, ROUND * P], U8, align_bytes=64)
                 nc.vector.quantize_mx(
-                    out=h_codes[:].bitcast(FP8X4),
-                    scales=h_scales[:],
-                    in_=live["h_grouped", r][:].rearrange("p g n t -> p (g n t)"),
+                    out=codes[:, first : last + 1, :].rearrange("p s n -> p (s n)").bitcast(FP8X4),
+                    scales=scales[:, first : last + 1, :].rearrange("p s n -> p (s n)"),
+                    in_=live["to_quantise", i][:, first : last + 1, :].rearrange("p s n -> p (s n)"),
                 )
-                live["h_mx", r] = (h_codes, h_scales)
+                live["h_mx", i] = (codes[:, 0, :], scales[:, 0, :])
+                live["g_mx", i - G_LAG] = (codes[:, 1, :], scales[:, 1, :])
 
             def layer_1(r):
                 h_codes, h_scales = live["h_mx", r]
@@ -189,8 +200,8 @@ def tile_ensembleenvprob_pa_t_e_kernel(
                         out=x_ps[:],
                         lhsT=wh_words[:, e, t * P : (t + 1) * P].bitcast(FP8X4),
                         lhsT_scale=wh_planes[:, e, t * P : (t + 1) * P],
-                        rhs=h_codes[:].bitcast(FP8X4),
-                        rhs_scale=h_scales[:],
+                        rhs=h_codes.bitcast(FP8X4),
+                        rhs_scale=h_scales,
                         start=True,
                         stop=True,
                     )
@@ -206,19 +217,10 @@ def tile_ensembleenvprob_pa_t_e_kernel(
                 live["g_planes", r] = g_planes
 
             def interleave_g(r):
-                g_grouped = work.tile([P, ROUND * P, PACK], BF16, align_bytes=64)
-                nc.vector.tensor_copy(out=g_grouped[:], in_=live["g_planes", r][:].rearrange("p t n -> p n t"))
-                live["g_grouped", r] = g_grouped
-
-            def quantise_g(r):
-                g_codes = work.tile([P, ROUND * P], U32, align_bytes=64)
-                g_scales = work.tile([P, ROUND * P], U8, align_bytes=64)
-                nc.vector.quantize_mx(
-                    out=g_codes[:].bitcast(FP8X4),
-                    scales=g_scales[:],
-                    in_=live["g_grouped", r][:].rearrange("p n t -> p (n t)"),
+                nc.vector.tensor_copy(
+                    out=live["to_quantise", r + G_LAG][:, 1, :].rearrange("p (c i t) -> p c t i", i=RUN, t=PACK),
+                    in_=live["g_planes", r][:].rearrange("p t (c i) -> p c t i", i=RUN),
                 )
-                live["g_mx", r] = (g_codes, g_scales)
 
             def heads(r):
                 g_codes, g_scales = live["g_mx", r]
@@ -228,8 +230,8 @@ def tile_ensembleenvprob_pa_t_e_kernel(
                     out=sigT_ps[:].rearrange("o g n -> o (g n)"),
                     lhsT=wsig_words[:, e, :].bitcast(FP8X4),
                     lhsT_scale=wsig_planes[:, e, :],
-                    rhs=g_codes[:].bitcast(FP8X4),
-                    rhs_scale=g_scales[:],
+                    rhs=g_codes.bitcast(FP8X4),
+                    rhs_scale=g_scales,
                     start=True,
                     stop=True,
                 )
@@ -282,12 +284,12 @@ def tile_ensembleenvprob_pa_t_e_kernel(
 
             def regroup_wh(e):
                 nc.vector.tensor_copy(
-                    out=wh_planes[:, e, :].rearrange("p (t m) -> p t m", t=PACK),
-                    in_=wh_raw_planes[:, e, :].rearrange("p (m t) -> p t m", t=PACK),
-                )
-                nc.vector.tensor_copy(
                     out=wh_words[:, e, :].rearrange("p (t m) -> p t m", t=PACK),
                     in_=wh_raw[:, e, :].bitcast(I32).rearrange("p (m t) -> p t m", t=PACK),
+                )
+                nc.vector.tensor_copy(
+                    out=wh_planes[:, e, :].rearrange("p (t m) -> p t m", t=PACK),
+                    in_=wh_raw_planes[:, e, :].rearrange("p (m t) -> p t m", t=PACK),
                 )
 
             bh_cols = keep.tile([P, MEMBERS, PACK], F32)
@@ -305,44 +307,48 @@ def tile_ensembleenvprob_pa_t_e_kernel(
                 nc.vector.tensor_copy(out=cols[:], in_=cols_ps[:, 0:8])
                 hi_lo = keep.tile([P, 2], F32)
                 nc.vector.tensor_tensor(out=hi_lo[:], in0=cols[:, 3:6:2], in1=cols[:, 4:7:2], op=ALU.add)
-                exp_hi_lo = keep.tile([P, 2], F32)
-                nc.scalar.activation(out=exp_hi_lo[:], in_=hi_lo[:], func=ACT.Exp)
-                live["constants"] = (cols, hi_lo, exp_hi_lo)
-
-            def finish_constants():
-                cols, hi_lo, exp_hi_lo = live["constants"]
                 half_hi = keep.tile([P, 1], F32)
                 nc.vector.tensor_scalar(out=half_hi[:], in0=hi_lo[:, 0:1], scalar1=0.5, scalar2=None, op0=ALU.mult)
                 nc.vector.tensor_scalar(
                     out=tanh_bias[:], in0=cols[:, 0:MEMBERS], scalar1=half_hi[:, 0:1], scalar2=None, op0=ALU.subtract
                 )
-                nc.vector.tensor_scalar(
+                powers = keep.tile([P, 2], F32)
+                nc.vector.tensor_scalar(out=powers[:], in0=hi_lo[:], scalar1=math.log2(math.e), scalar2=None, op0=ALU.mult)
+                two = keep.tile([P, 2], F32)
+                nc.gpsimd.memset(two[:], 2.0)
+                exp_hi_lo = keep.tile([P, 2], F32)
+                nc.gpsimd.tensor_tensor(out=exp_hi_lo[:], in0=two[:], in1=powers[:], op=ALU.pow)
+                nc.gpsimd.tensor_scalar(
                     out=sqrt_scale[:], in0=exp_hi_lo[:, 0:1], scalar1=0.5, scalar2=None, op0=ALU.mult
                 )
-                nc.vector.tensor_tensor(out=sqrt_bias[:], in0=sqrt_scale[:], in1=exp_hi_lo[:, 1:2], op=ALU.add)
+                nc.gpsimd.tensor_tensor(out=sqrt_bias[:], in0=sqrt_scale[:], in1=exp_hi_lo[:, 1:2], op=ALU.add)
                 nc.vector.tensor_copy(out=bmu_f32[:], in_=bmu_bf[:])
 
             nc.vector.tensor_copy(out=bh_cols[:], in_=bh_bf[:])
             regroup_wh(0)
-            for i in range(ROUNDS + 4):
-                run(add_bmu, i - 4)
-                run(tanh_sigma, i - 4)
+            for i in range(ROUNDS + G_LAG + 2):
+                if i < ROUNDS + G_LAG:
+                    new_step(i)
+                run(tanh_sigma, i - G_LAG - 2)
                 run(transpose_h, i)
+                run(interleave_g, i - G_LAG)
                 run(regroup_h, i)
+                run(add_bmu, i - G_LAG - 2)
+                if i < ROUNDS + G_LAG:
+                    quantise(i)
                 if i == 0:
-                    prepare_constants()
-                run(interleave_g, i - 2)
-                run(quantise_h, i)
-                run(quantise_g, i - 2)
-                run(layer_1, i - 1)
-                run(swish, i - 1)
-                run(heads, i - 3)
+                    layer_1(0)
+                    swish(0)
+                elif i > 1:
+                    run(layer_1, i - 1)
+                    run(swish, i - 1)
+                run(heads, i - G_LAG - 1)
                 if i + AHEAD < ROUNDS:
                     load_h(i + AHEAD)
                 if i in (0, 1):
                     regroup_wh(i + 1)
-                if i == 1:
-                    finish_constants()
+                if i == 2:
+                    prepare_constants()
 
         with tc.psum_pool(name="psum_sg", bufs=4) as psum_sg:
             for first in range(0, BLOCKS, SQRT_BLOCKS):
@@ -358,10 +364,13 @@ def tile_ensembleenvprob_pa_t_e_kernel(
                 sg_ps = psum_sg.tile([P, SQRT_BLOCKS, OUT], F32)
                 for g in range(SQRT_BLOCKS):
                     nc.tensor.transpose(out=sg_ps[:, g, :], in_=sgT[:, g, :], identity=ident[:])
-                sg_state = results.tile([P, SQRT_BLOCKS, STATE], F32, bufs=8)
-                nc.vector.tensor_copy(out=sg_state[:], in_=sg_ps[:, :, 0:STATE])
+                part = first % STORE_BLOCKS
+                if part == 0:
+                    sg_state = results.tile([P, STORE_BLOCKS, STATE], F32, bufs=4)
+                nc.vector.tensor_copy(out=sg_state[:, part : part + SQRT_BLOCKS, :], in_=sg_ps[:, :, 0:STATE])
                 nc.vector.tensor_copy(out=sg_reward[:, blocks, :], in_=sg_ps[:, :, STATE:OUT])
-                nc.sync.dma_start(out=ds_sg[:, blocks, :], in_=sg_state[:])
+                if blocks.stop % STORE_BLOCKS == 0:
+                    nc.sync.dma_start(out=ds_sg[:, blocks.stop - STORE_BLOCKS : blocks.stop, :], in_=sg_state[:])
                 if blocks.stop % REWARD_BLOCKS == 0:
                     stored = slice(blocks.stop - REWARD_BLOCKS, blocks.stop)
                     nc.sync.dma_start(out=r_sg[:, stored, :], in_=sg_reward[:, stored, :])

@@ -23,8 +23,9 @@ REWARD = OUT - STATE
 BLOCKS = 96
 ROUND = 4
 ROUNDS = BLOCKS // ROUND
+ALL = slice(0, ROUND)
+HALVES = (slice(0, ROUND // 2), slice(ROUND // 2, ROUND))
 G_LAG = 3
-SCALAR_LAST = 5
 RUN = 4
 AHEAD = 8
 GROUP = ROUND * MEMBERS
@@ -81,8 +82,8 @@ def tile_ensembleenvprob_pa_t_e_kernel(
     r_mu = out_2.flatten_outer_dims().rearrange("(p b) o -> p b o", b=BLOCKS)
     r_sg = out_3.flatten_outer_dims().rearrange("(p b) o -> p b o", b=BLOCKS)
 
-    def blocks_from(first):
-        return slice(first, first + MEMBERS * (ROUND - 1) + 1, MEMBERS)
+    def blocks_from(first, blocks=ALL):
+        return slice(first + MEMBERS * blocks.start, first + MEMBERS * (blocks.stop - 1) + 1, MEMBERS)
 
     def first_block(r):
         return GROUP * (r // MEMBERS) + r % MEMBERS
@@ -119,8 +120,8 @@ def tile_ensembleenvprob_pa_t_e_kernel(
 
         load_h(0, parts=2)
         load_words(nc, wh_raw, Wh_words, slice(0, 1))
-        wh_raw_planes = load_scales(nc, keep, Wh_scales, HID, "wh_raw")
         load_h(1)
+        wh_raw_planes = load_scales(nc, keep, Wh_scales, HID, "wh_raw")
         load_words(nc, wh_raw, Wh_words, slice(1, 2))
         load_h(2)
         load_words(nc, wh_raw, Wh_words, slice(2, 3))
@@ -166,7 +167,7 @@ def tile_ensembleenvprob_pa_t_e_kernel(
 
             def regroup_h(r):
                 h_grouped = live["to_quantise", r][:, 0, :].rearrange("p (g n t) -> p g n t", g=ROUND, t=PACK)
-                second = nc.scalar.copy if r == 0 or r >= ROUNDS - SCALAR_LAST else nc.vector.tensor_copy
+                second = nc.scalar.copy if r == 0 else nc.vector.tensor_copy
                 for half, copy in enumerate((nc.scalar.copy, second)):
                     blocks = slice(half * ROUND // 2, (half + 1) * ROUND // 2)
                     copy(
@@ -183,16 +184,36 @@ def tile_ensembleenvprob_pa_t_e_kernel(
                 last = 1 if i >= G_LAG else 0
                 codes = work.tile([P, 2, ROUND * P], U32, align_bytes=64)
                 scales = work.tile([P, 2, ROUND * P], U8, align_bytes=64)
-                nc.vector.quantize_mx(
-                    out=codes[:, first : last + 1, :].rearrange("p s n -> p (s n)").bitcast(FP8X4),
-                    scales=scales[:, first : last + 1, :].rearrange("p s n -> p (s n)"),
-                    in_=live["to_quantise", i][:, first : last + 1, :].rearrange("p s n -> p (s n)"),
+                live["codes", i] = (codes, scales)
+                quantise_columns(
+                    codes[:, first : last + 1, :].rearrange("p s n -> p (s n)"),
+                    scales[:, first : last + 1, :].rearrange("p s n -> p (s n)"),
+                    live["to_quantise", i][:, first : last + 1, :].rearrange("p s n -> p (s n)"),
                 )
-                live["h_mx", i] = (codes[:, 0, :], scales[:, 0, :])
-                live["g_mx", i - G_LAG] = (codes[:, 1, :], scales[:, 1, :])
+
+            def quantise_columns(codes, scales, values):
+                nc.vector.quantize_mx(out=codes.bitcast(FP8X4), scales=scales, in_=values)
+
+            def quantise_last_g(blocks):
+                i = ROUNDS - 1 + G_LAG
+                if blocks.start == 0:
+                    codes = work.tile([P, 2, ROUND * P], U32, align_bytes=64)
+                    scales = work.tile([P, 2, ROUND * P], U8, align_bytes=64)
+                    live["codes", i] = (codes, scales)
+                codes, scales = live["codes", i]
+                columns = slice(blocks.start * P, blocks.stop * P)
+                quantise_columns(
+                    codes[:, 1, columns],
+                    scales[:, 1, columns],
+                    live["to_quantise", i][:, 1, blocks.start * P * PACK : blocks.stop * P * PACK],
+                )
+
+            def mx_operand(i, part):
+                codes, scales = live["codes", i]
+                return codes[:, part, :], scales[:, part, :]
 
             def layer_1(r):
-                h_codes, h_scales = live["h_mx", r]
+                h_codes, h_scales = mx_operand(r, 0)
                 e = r % MEMBERS
                 for t in range(PACK):
                     x_ps = psum.tile([P, ROUND * P], F32, tag="x_ps%d" % t)
@@ -207,38 +228,49 @@ def tile_ensembleenvprob_pa_t_e_kernel(
                     )
                     live["x_ps", r, t] = x_ps
 
-            def swish(r):
+            def swish(r, blocks=ALL):
                 e = r % MEMBERS
-                g_planes = work.tile([P, PACK, ROUND * P], BF16, align_bytes=64)
+                if blocks.start == 0:
+                    g_planes = work.tile([P, PACK, ROUND * P], BF16, align_bytes=64)
+                    live["g_planes", r] = g_planes
+                rows = slice(blocks.start * P, blocks.stop * P)
                 for t in range(PACK):
                     nc.scalar.activation(
-                        out=g_planes[:, t, :], in_=live["x_ps", r, t][:], func=ACT.Silu, bias=bh_cols[:, e, t : t + 1]
+                        out=live["g_planes", r][:, t, rows],
+                        in_=live["x_ps", r, t][:, rows],
+                        func=ACT.Silu,
+                        bias=bh_cols[:, e, t : t + 1],
                     )
-                live["g_planes", r] = g_planes
 
-            def interleave_g(r):
+            def interleave_g(r, blocks=ALL):
+                rows = slice(blocks.start * P, blocks.stop * P)
+                values = slice(blocks.start * P * PACK, blocks.stop * P * PACK)
                 nc.vector.tensor_copy(
-                    out=live["to_quantise", r + G_LAG][:, 1, :].rearrange("p (c i t) -> p c t i", i=RUN, t=PACK),
-                    in_=live["g_planes", r][:].rearrange("p t (c i) -> p c t i", i=RUN),
+                    out=live["to_quantise", r + G_LAG][:, 1, values].rearrange("p (c i t) -> p c t i", i=RUN, t=PACK),
+                    in_=live["g_planes", r][:, :, rows].rearrange("p t (c i) -> p c t i", i=RUN),
                 )
 
-            def heads(r):
-                g_codes, g_scales = live["g_mx", r]
+            def heads(r, blocks=ALL):
+                g_codes, g_scales = mx_operand(r + G_LAG, 1)
                 e = r % MEMBERS
-                sigT_ps = psum.tile([P, ROUND, P], F32)
+                if blocks.start == 0:
+                    sigT_ps = psum.tile([P, ROUND, P], F32)
+                    mu_ps = psum.tile([P, ROUND, OUT], F32)
+                    live["mu_ps", r] = mu_ps
+                    live["sigT_ps", r] = sigT_ps
+                rows = slice(blocks.start * P, blocks.stop * P)
                 nc.tensor.matmul_mx(
-                    out=sigT_ps[:].rearrange("o g n -> o (g n)"),
+                    out=live["sigT_ps", r][:, blocks, :].rearrange("o g n -> o (g n)"),
                     lhsT=wsig_words[:, e, :].bitcast(FP8X4),
                     lhsT_scale=wsig_planes[:, e, :],
-                    rhs=g_codes.bitcast(FP8X4),
-                    rhs_scale=g_scales,
+                    rhs=g_codes[:, rows].bitcast(FP8X4),
+                    rhs_scale=g_scales[:, rows],
                     start=True,
                     stop=True,
                 )
-                mu_ps = psum.tile([P, ROUND, OUT], F32)
-                for g in range(ROUND):
+                for g in range(blocks.start, blocks.stop):
                     nc.tensor.matmul_mx(
-                        out=mu_ps[:, g, :],
+                        out=live["mu_ps", r][:, g, :],
                         lhsT=g_codes[:, g * P : (g + 1) * P].bitcast(FP8X4),
                         lhsT_scale=g_scales[:, g * P : (g + 1) * P],
                         rhs=wmu_words[:, e, :].bitcast(FP8X4),
@@ -246,14 +278,12 @@ def tile_ensembleenvprob_pa_t_e_kernel(
                         start=True,
                         stop=True,
                     )
-                live["mu_ps", r] = mu_ps
-                live["sigT_ps", r] = sigT_ps
 
-            def tanh_sigma(r):
+            def tanh_sigma(r, blocks=ALL):
                 e = r % MEMBERS
                 nc.scalar.activation(
-                    out=tanh_all[:, blocks_from(first_block(r)), :],
-                    in_=live["sigT_ps", r][:],
+                    out=tanh_all[:, blocks_from(first_block(r), blocks), :],
+                    in_=live["sigT_ps", r][:, blocks, :],
                     func=ACT.Tanh,
                     bias=tanh_bias[:, e : e + 1],
                 )
@@ -326,21 +356,16 @@ def tile_ensembleenvprob_pa_t_e_kernel(
 
             nc.vector.tensor_copy(out=bh_cols[:], in_=bh_bf[:])
             regroup_wh(0)
-            for i in range(ROUNDS + G_LAG + 2):
-                if i < ROUNDS + G_LAG:
-                    new_step(i)
+            for i in range(ROUNDS + G_LAG - 1):
+                new_step(i)
                 run(tanh_sigma, i - G_LAG - 2)
                 run(transpose_h, i)
                 run(interleave_g, i - G_LAG)
                 run(regroup_h, i)
                 run(add_bmu, i - G_LAG - 2)
-                if i < ROUNDS + G_LAG:
-                    quantise(i)
-                if i == 0:
-                    layer_1(0)
-                    swish(0)
-                elif i > 1:
-                    run(layer_1, i - 1)
+                quantise(i)
+                run(layer_1, i - 1)
+                if i < ROUNDS:
                     run(swish, i - 1)
                 run(heads, i - G_LAG - 1)
                 if i + AHEAD < ROUNDS:
@@ -349,6 +374,24 @@ def tile_ensembleenvprob_pa_t_e_kernel(
                     regroup_wh(i + 1)
                 if i == 2:
                     prepare_constants()
+                if i == ROUNDS:
+                    for blocks in HALVES:
+                        swish(ROUNDS - 1, blocks)
+            r = ROUNDS - 1
+            new_step(r + G_LAG)
+            tanh_sigma(r - 2)
+            interleave_g(r, HALVES[0])
+            add_bmu(r - 2)
+            quantise_last_g(HALVES[0])
+            heads(r - 1)
+            tanh_sigma(r - 1)
+            interleave_g(r, HALVES[1])
+            add_bmu(r - 1)
+            quantise_last_g(HALVES[1])
+            for blocks in HALVES:
+                heads(r, blocks)
+                tanh_sigma(r, blocks)
+            add_bmu(r)
 
         with tc.psum_pool(name="psum_sg", bufs=4) as psum_sg:
             for first in range(0, BLOCKS, SQRT_BLOCKS):

@@ -27,6 +27,7 @@ ALL = slice(0, ROUND)
 HALVES = (slice(0, ROUND // 2), slice(ROUND // 2, ROUND))
 G_LAG = 3
 RUN = 4
+SCALAR_BOTH = 5
 AHEAD = 8
 GROUP = ROUND * MEMBERS
 REWARD_BLOCKS = 24
@@ -125,22 +126,24 @@ def tile_ensembleenvprob_pa_t_e_kernel(
         load_words(nc, wh_raw, Wh_words, slice(1, 2))
         load_h(2)
         load_words(nc, wh_raw, Wh_words, slice(2, 3))
-        nc.sync.dma_start(out=rows_bf[0:MEMBERS, :], in_=bsig)
-        nc.sync.dma_start(out=rows_bf[3:4, 0:STATE], in_=max_lv_s)
-        nc.sync.dma_start(out=rows_bf[4:5, STATE:OUT], in_=max_lv_r)
-        nc.sync.dma_start(out=rows_bf[5:6, 0:STATE], in_=min_lv_s)
-        nc.sync.dma_start(out=rows_bf[6:7, STATE:OUT], in_=min_lv_r)
+        load_h(3)
+        load_h(4)
         wmu_planes = load_scales(nc, keep, Wmu_scales, OUT, "wmu")
         wsig_planes = load_scales(nc, keep, Wsig_scales, OUT, "wsig")
         load_words(nc, wmu_words, Wmu_words, everyone)
         load_words(nc, wsig_words, Wsig_words, everyone)
-        for r in range(MEMBERS, AHEAD):
+        for r in range(5, AHEAD):
             load_h(r)
 
         bh_bf = keep.tile([P, MEMBERS, PACK], BF16)
         nc.scalar.dma_start(out=bh_bf[:], in_=bh.rearrange("e (p t) -> p e t", t=PACK))
+        nc.gpsimd.dma_start(out=rows_bf[0:MEMBERS, :], in_=bsig)
+        nc.gpsimd.dma_start(out=rows_bf[3:4, 0:STATE], in_=max_lv_s)
+        nc.gpsimd.dma_start(out=rows_bf[4:5, STATE:OUT], in_=max_lv_r)
+        nc.gpsimd.dma_start(out=rows_bf[5:6, 0:STATE], in_=min_lv_s)
+        nc.gpsimd.dma_start(out=rows_bf[6:7, STATE:OUT], in_=min_lv_r)
         bmu_bf = keep.tile([P, MEMBERS, OUT], BF16)
-        nc.scalar.dma_start(
+        nc.gpsimd.dma_start(
             out=bmu_bf[:].rearrange("n e o -> n (e o)"),
             in_=bmu.rearrange("e o -> (e o)").partition_broadcast(P),
         )
@@ -167,7 +170,7 @@ def tile_ensembleenvprob_pa_t_e_kernel(
 
             def regroup_h(r):
                 h_grouped = live["to_quantise", r][:, 0, :].rearrange("p (g n t) -> p g n t", g=ROUND, t=PACK)
-                second = nc.scalar.copy if r == 0 else nc.vector.tensor_copy
+                second = nc.scalar.copy if r % SCALAR_BOTH == 0 else nc.vector.tensor_copy
                 for half, copy in enumerate((nc.scalar.copy, second)):
                     blocks = slice(half * ROUND // 2, (half + 1) * ROUND // 2)
                     copy(
@@ -254,8 +257,9 @@ def tile_ensembleenvprob_pa_t_e_kernel(
                 g_codes, g_scales = mx_operand(r + G_LAG, 1)
                 e = r % MEMBERS
                 if blocks.start == 0:
-                    sigT_ps = psum.tile([P, ROUND, P], F32)
-                    mu_ps = psum.tile([P, ROUND, OUT], F32)
+                    spare = ROUNDS - 1 - r
+                    sigT_ps = psum.tile([P, ROUND, P], F32, tag="x_ps%d" % spare if spare < 2 else "sigT_ps")
+                    mu_ps = psum.tile([P, ROUND, OUT], F32, tag="x_ps%d" % (spare + 2) if spare < 2 else "mu_ps")
                     live["mu_ps", r] = mu_ps
                     live["sigT_ps", r] = sigT_ps
                 rows = slice(blocks.start * P, blocks.stop * P)
@@ -379,19 +383,17 @@ def tile_ensembleenvprob_pa_t_e_kernel(
                         swish(ROUNDS - 1, blocks)
             r = ROUNDS - 1
             new_step(r + G_LAG)
-            tanh_sigma(r - 2)
             interleave_g(r, HALVES[0])
-            add_bmu(r - 2)
-            quantise_last_g(HALVES[0])
             heads(r - 1)
-            tanh_sigma(r - 1)
+            tanh_sigma(r - 2)
             interleave_g(r, HALVES[1])
-            add_bmu(r - 1)
-            quantise_last_g(HALVES[1])
+            tanh_sigma(r - 1)
             for blocks in HALVES:
+                quantise_last_g(blocks)
                 heads(r, blocks)
                 tanh_sigma(r, blocks)
-            add_bmu(r)
+            for late in (r - 2, r - 1, r):
+                add_bmu(late)
 
         with tc.psum_pool(name="psum_sg", bufs=4) as psum_sg:
             for first in range(0, BLOCKS, SQRT_BLOCKS):
@@ -407,13 +409,15 @@ def tile_ensembleenvprob_pa_t_e_kernel(
                 sg_ps = psum_sg.tile([P, SQRT_BLOCKS, OUT], F32)
                 for g in range(SQRT_BLOCKS):
                     nc.tensor.transpose(out=sg_ps[:, g, :], in_=sgT[:, g, :], identity=ident[:])
-                part = first % STORE_BLOCKS
+                width = STORE_BLOCKS if STORE_BLOCKS <= first < BLOCKS - STORE_BLOCKS else SQRT_BLOCKS
+                copy = nc.vector.tensor_copy if first < BLOCKS - SQRT_BLOCKS else nc.scalar.copy
+                part = first % width
                 if part == 0:
-                    sg_state = results.tile([P, STORE_BLOCKS, STATE], F32, bufs=4)
-                nc.vector.tensor_copy(out=sg_state[:, part : part + SQRT_BLOCKS, :], in_=sg_ps[:, :, 0:STATE])
-                nc.vector.tensor_copy(out=sg_reward[:, blocks, :], in_=sg_ps[:, :, STATE:OUT])
-                if blocks.stop % STORE_BLOCKS == 0:
-                    nc.sync.dma_start(out=ds_sg[:, blocks.stop - STORE_BLOCKS : blocks.stop, :], in_=sg_state[:])
+                    sg_state = results.tile([P, STORE_BLOCKS, STATE], F32, bufs=6)
+                copy(out=sg_state[:, part : part + SQRT_BLOCKS, :], in_=sg_ps[:, :, 0:STATE])
+                copy(out=sg_reward[:, blocks, :], in_=sg_ps[:, :, STATE:OUT])
+                if blocks.stop % width == 0:
+                    nc.sync.dma_start(out=ds_sg[:, blocks.stop - width : blocks.stop, :], in_=sg_state[:, 0:width, :])
                 if blocks.stop % REWARD_BLOCKS == 0:
                     stored = slice(blocks.stop - REWARD_BLOCKS, blocks.stop)
                     nc.sync.dma_start(out=r_sg[:, stored, :], in_=sg_reward[:, stored, :])

import math
from contextlib import ExitStack

import concourse.mybir as mybir
from concourse.masks import make_identity

F32 = mybir.dt.float32
BF16 = mybir.dt.bfloat16
I32 = mybir.dt.int32
U32 = mybir.dt.uint32
U8 = mybir.dt.uint8
FP8X4 = mybir.dt.float8_e4m3fn_x4
ACT = mybir.ActivationFunctionType
ALU = mybir.AluOpType

P = 128
PACK = 4
MEMBERS = 3
HID = 512
OUT = 128
STATE = 120
REWARD = OUT - STATE
BLOCKS = 96
ROUND = 4
ROUNDS = BLOCKS // ROUND
ALL = slice(0, ROUND)
HALVES = (slice(0, ROUND // 2), slice(ROUND // 2, ROUND))
G_LAG = 3
RUN = 4
SCALAR_BOTH = 5
AHEAD = 8
GROUP = ROUND * MEMBERS
REWARD_BLOCKS = 24
SQRT_BLOCKS = 4
STORE_BLOCKS = 8

FLOPS = 2 * 4096 * MEMBERS * (HID * HID + 2 * HID * OUT)


def load_scales(nc, pool, scales_dram, width, label):
    planes = pool.tile([P, MEMBERS, width], U8, name=label + "_planes", align_bytes=64)
    nc.vector.memset(planes[:].bitcast(I32), 0)
    for quadrant in range(4):
        nc.sync.dma_start(
            out=planes[32 * quadrant : 32 * quadrant + 4].bitcast(I32),
            in_=scales_dram[:, 4 * quadrant : 4 * quadrant + 4, :].rearrange("e r n -> r e n").bitcast(I32),
        )
    return planes


def load_words(nc, words, words_dram, members):
    nc.sync.dma_start(
        out=words[:, members, :].bitcast(I32),
        in_=words_dram[members].rearrange("e p n t -> p e (n t)").bitcast(I32),
    )


def tile_ensembleenvprob_pa_t_e_kernel(
    tc,
    h,
    Wh_words,
    Wh_scales,
    bh,
    Wmu_words,
    Wmu_scales,
    bmu,
    Wsig_words,
    Wsig_scales,
    bsig,
    max_lv_s,
    min_lv_s,
    max_lv_r,
    min_lv_r,
    out_0,
    out_1,
    out_2,
    out_3,
):
    nc = tc.nc
    h_blocks = h.flatten_outer_dims().rearrange("(p b) k -> p b k", b=BLOCKS)
    ds_mu = out_0.flatten_outer_dims().rearrange("(p b) o -> p b o", b=BLOCKS)
    ds_sg = out_1.flatten_outer_dims().rearrange("(p b) o -> p b o", b=BLOCKS)
    r_mu = out_2.flatten_outer_dims().rearrange("(p b) o -> p b o", b=BLOCKS)
    r_sg = out_3.flatten_outer_dims().rearrange("(p b) o -> p b o", b=BLOCKS)

    def blocks_from(first, blocks=ALL):
        return slice(first + MEMBERS * blocks.start, first + MEMBERS * (blocks.stop - 1) + 1, MEMBERS)

    def first_block(r):
        return GROUP * (r // MEMBERS) + r % MEMBERS

    with ExitStack() as stack:
        stack.enter_context(tc.manual_schedule())
        keep = stack.enter_context(tc.tile_pool(name="keep", bufs=1))
        work = stack.enter_context(tc.tile_pool(name="work", bufs=3))
        results = stack.enter_context(tc.tile_pool(name="results", bufs=3))
        loads = stack.enter_context(tc.tile_pool(name="loads", bufs=AHEAD))

        rows_bf = keep.tile([P, P], BF16)
        nc.vector.memset(rows_bf[:], 0.0)
        ident = keep.tile([P, P], F32)
        make_identity(nc, ident[:])

        h_tiles = {}

        def load_h(r, parts=1):
            h_tile = loads.tile([P, ROUND, HID], BF16)
            for part in range(parts):
                first = part * ROUND // parts
                last = (part + 1) * ROUND // parts - 1
                nc.sync.dma_start(
                    out=h_tile[:, first : last + 1, :],
                    in_=h_blocks[:, first_block(r) + MEMBERS * first : first_block(r) + MEMBERS * last + 1 : MEMBERS, :],
                )
            h_tiles[r] = h_tile

        wh_raw = keep.tile([P, MEMBERS, PACK * HID], U8, align_bytes=64)
        wmu_words = keep.tile([P, MEMBERS, PACK * OUT], U8, align_bytes=64)
        wsig_words = keep.tile([P, MEMBERS, PACK * OUT], U8, align_bytes=64)
        everyone = slice(0, MEMBERS)

        load_h(0, parts=2)
        load_words(nc, wh_raw, Wh_words, slice(0, 1))
        load_h(1)
        wh_raw_planes = load_scales(nc, keep, Wh_scales, HID, "wh_raw")
        load_words(nc, wh_raw, Wh_words, slice(1, 2))
        load_h(2)
        load_words(nc, wh_raw, Wh_words, slice(2, 3))
        load_h(3)
        load_h(4)
        wmu_planes = load_scales(nc, keep, Wmu_scales, OUT, "wmu")
        wsig_planes = load_scales(nc, keep, Wsig_scales, OUT, "wsig")
        load_words(nc, wmu_words, Wmu_words, everyone)
        load_words(nc, wsig_words, Wsig_words, everyone)
        for r in range(5, AHEAD):
            load_h(r)

        bh_bf = keep.tile([P, MEMBERS, PACK], BF16)
        nc.scalar.dma_start(out=bh_bf[:], in_=bh.rearrange("e (p t) -> p e t", t=PACK))
        nc.gpsimd.dma_start(out=rows_bf[0:MEMBERS, :], in_=bsig)
        nc.gpsimd.dma_start(out=rows_bf[3:4, 0:STATE], in_=max_lv_s)
        nc.gpsimd.dma_start(out=rows_bf[4:5, STATE:OUT], in_=max_lv_r)
        nc.gpsimd.dma_start(out=rows_bf[5:6, 0:STATE], in_=min_lv_s)
        nc.gpsimd.dma_start(out=rows_bf[6:7, STATE:OUT], in_=min_lv_r)
        bmu_bf = keep.tile([P, MEMBERS, OUT], BF16)
        nc.gpsimd.dma_start(
            out=bmu_bf[:].rearrange("n e o -> n (e o)"),
            in_=bmu.rearrange("e o -> (e o)").partition_broadcast(P),
        )
        idle = keep.tile([P, 1], F32)
        nc.vector.memset(idle[:], 0.0)
        nc.scalar.activation(out=idle[:], in_=idle[:], func=ACT.Silu)

        tanh_all = keep.tile([P, BLOCKS, P], F32)
        sg_reward = keep.tile([P, BLOCKS, REWARD], F32)

        with tc.psum_pool(name="psum", bufs=1) as psum:
            live = {}

            def transpose_h(r):
                halves = []
                for half in range(2):
                    hT = psum.tile([P, ROUND // 2, 2, P], F32, tag="hT%d" % half)
                    for g in range(ROUND // 2):
                        words = h_tiles[r][:, half * ROUND // 2 + g, :].bitcast(F32)
                        for u in range(2):
                            nc.tensor.transpose(out=hT[:, g, u, :], in_=words[:, u : HID // 2 : 2], identity=ident[:])
                    halves.append(hT)
                live["hT", r] = halves

            def regroup_h(r):
                h_grouped = live["to_quantise", r][:, 0, :].rearrange("p (g n t) -> p g n t", g=ROUND, t=PACK)
                second = nc.scalar.copy if r % SCALAR_BOTH == 0 else nc.vector.tensor_copy
                for half, copy in enumerate((nc.scalar.copy, second)):
                    blocks = slice(half * ROUND // 2, (half + 1) * ROUND // 2)
                    copy(
                        out=h_grouped[:, blocks].rearrange("p g n t -> p (g n t)").bitcast(F32).rearrange("p (g n u) -> p g n u", g=ROUND // 2, u=2),
                        in_=live["hT", r][half][:].rearrange("p g u n -> p g n u"),
                    )

            def new_step(i):
                to_quantise = work.tile([P, 2, ROUND * P * PACK], BF16, align_bytes=64)
                live["to_quantise", i] = to_quantise

            def quantise(i):
                first = 0 if i < ROUNDS else 1
                last = 1 if i >= G_LAG else 0
                codes = work.tile([P, 2, ROUND * P], U32, align_bytes=64)
                scales = work.tile([P, 2, ROUND * P], U8, align_bytes=64)
                live["codes", i] = (codes, scales)
                quantise_columns(
                    codes[:, first : last + 1, :].rearrange("p s n -> p (s n)"),
                    scales[:, first : last + 1, :].rearrange("p s n -> p (s n)"),
                    live["to_quantise", i][:, first : last + 1, :].rearrange("p s n -> p (s n)"),
                )

            def quantise_columns(codes, scales, values):
                nc.vector.quantize_mx(out=codes.bitcast(FP8X4), scales=scales, in_=values)

            def quantise_last_g(blocks):
                i = ROUNDS - 1 + G_LAG
                if blocks.start == 0:
                    codes = work.tile([P, 2, ROUND * P], U32, align_bytes=64)
                    scales = work.tile([P, 2, ROUND * P], U8, align_bytes=64)
                    live["codes", i] = (codes, scales)
                codes, scales = live["codes", i]
                columns = slice(blocks.start * P, blocks.stop * P)
                quantise_columns(
                    codes[:, 1, columns],
                    scales[:, 1, columns],
                    live["to_quantise", i][:, 1, blocks.start * P * PACK : blocks.stop * P * PACK],
                )

            def mx_operand(i, part):
                codes, scales = live["codes", i]
                return codes[:, part, :], scales[:, part, :]

            def layer_1(r):
                h_codes, h_scales = mx_operand(r, 0)
                e = r % MEMBERS
                for t in range(PACK):
                    x_ps = psum.tile([P, ROUND * P], F32, tag="x_ps%d" % t)
                    nc.tensor.matmul_mx(
                        out=x_ps[:],
                        lhsT=wh_words[:, e, t * P : (t + 1) * P].bitcast(FP8X4),
                        lhsT_scale=wh_planes[:, e, t * P : (t + 1) * P],
                        rhs=h_codes.bitcast(FP8X4),
                        rhs_scale=h_scales,
                        start=True,
                        stop=True,
                    )
                    live["x_ps", r, t] = x_ps

            def swish(r, blocks=ALL):
                e = r % MEMBERS
                if blocks.start == 0:
                    g_planes = work.tile([P, PACK, ROUND * P], BF16, align_bytes=64)
                    live["g_planes", r] = g_planes
                rows = slice(blocks.start * P, blocks.stop * P)
                for t in range(PACK):
                    nc.scalar.activation(
                        out=live["g_planes", r][:, t, rows],
                        in_=live["x_ps", r, t][:, rows],
                        func=ACT.Silu,
                        bias=bh_cols[:, e, t : t + 1],
                    )

            def interleave_g(r, blocks=ALL):
                rows = slice(blocks.start * P, blocks.stop * P)
                values = slice(blocks.start * P * PACK, blocks.stop * P * PACK)
                nc.vector.tensor_copy(
                    out=live["to_quantise", r + G_LAG][:, 1, values].rearrange("p (c i t) -> p c t i", i=RUN, t=PACK),
                    in_=live["g_planes", r][:, :, rows].rearrange("p t (c i) -> p c t i", i=RUN),
                )

            def heads(r, blocks=ALL):
                g_codes, g_scales = mx_operand(r + G_LAG, 1)
                e = r % MEMBERS
                if blocks.start == 0:
                    spare = ROUNDS - 1 - r
                    sigT_ps = psum.tile([P, ROUND, P], F32, tag="x_ps%d" % spare if spare < 2 else "sigT_ps")
                    mu_ps = psum.tile([P, ROUND, OUT], F32, tag="x_ps%d" % (spare + 2) if spare < 2 else "mu_ps")
                    live["mu_ps", r] = mu_ps
                    live["sigT_ps", r] = sigT_ps
                rows = slice(blocks.start * P, blocks.stop * P)
                nc.tensor.matmul_mx(
                    out=live["sigT_ps", r][:, blocks, :].rearrange("o g n -> o (g n)"),
                    lhsT=wsig_words[:, e, :].bitcast(FP8X4),
                    lhsT_scale=wsig_planes[:, e, :],
                    rhs=g_codes[:, rows].bitcast(FP8X4),
                    rhs_scale=g_scales[:, rows],
                    start=True,
                    stop=True,
                )
                for g in range(blocks.start, blocks.stop):
                    nc.tensor.matmul_mx(
                        out=live["mu_ps", r][:, g, :],
                        lhsT=g_codes[:, g * P : (g + 1) * P].bitcast(FP8X4),
                        lhsT_scale=g_scales[:, g * P : (g + 1) * P],
                        rhs=wmu_words[:, e, :].bitcast(FP8X4),
                        rhs_scale=wmu_planes[:, e, :],
                        start=True,
                        stop=True,
                    )

            def tanh_sigma(r, blocks=ALL):
                e = r % MEMBERS
                nc.scalar.activation(
                    out=tanh_all[:, blocks_from(first_block(r), blocks), :],
                    in_=live["sigT_ps", r][:, blocks, :],
                    func=ACT.Tanh,
                    bias=tanh_bias[:, e : e + 1],
                )

            def add_bmu(r):
                e = r % MEMBERS
                if e == 0:
                    mu_group = results.tile([P, GROUP, OUT], F32)
                    live["mu_sb"] = mu_group
                mu_sb = live["mu_sb"]
                nc.vector.tensor_tensor(
                    out=mu_sb[:, blocks_from(e), :],
                    in0=live["mu_ps", r][:],
                    in1=bmu_f32[:, e : e + 1, :].to_broadcast([P, ROUND, OUT]),
                    op=ALU.add,
                )
                if e == MEMBERS - 1:
                    stored = slice(r // MEMBERS * GROUP, (r // MEMBERS + 1) * GROUP)
                    nc.sync.dma_start(out=ds_mu[:, stored, :], in_=mu_sb[:, :, 0:STATE])
                    nc.sync.dma_start(out=r_mu[:, stored, :], in_=mu_sb[:, :, STATE:OUT])

            def run(stage, r):
                if 0 <= r < ROUNDS:
                    stage(r)

            wh_words = keep.tile([P, MEMBERS, HID], I32, align_bytes=64)
            wh_planes = keep.tile([P, MEMBERS, HID], U8, align_bytes=64)

            def regroup_wh(e):
                nc.vector.tensor_copy(
                    out=wh_words[:, e, :].rearrange("p (t m) -> p t m", t=PACK),
                    in_=wh_raw[:, e, :].bitcast(I32).rearrange("p (m t) -> p t m", t=PACK),
                )
                nc.vector.tensor_copy(
                    out=wh_planes[:, e, :].rearrange("p (t m) -> p t m", t=PACK),
                    in_=wh_raw_planes[:, e, :].rearrange("p (m t) -> p t m", t=PACK),
                )

            bh_cols = keep.tile([P, MEMBERS, PACK], F32)
            bmu_f32 = keep.tile([P, MEMBERS, OUT], F32)
            tanh_bias = keep.tile([P, MEMBERS], F32)
            sqrt_scale = keep.tile([P, 1], F32)
            sqrt_bias = keep.tile([P, 1], F32)

            def prepare_constants():
                rows_f32 = keep.tile([P, P], F32)
                nc.vector.tensor_copy(out=rows_f32[:], in_=rows_bf[:])
                cols_ps = psum.tile([P, P], F32, tag="mu_ps")
                nc.tensor.transpose(out=cols_ps[:], in_=rows_f32[:], identity=ident[:])
                cols = keep.tile([P, 8], F32)
                nc.vector.tensor_copy(out=cols[:], in_=cols_ps[:, 0:8])
                hi_lo = keep.tile([P, 2], F32)
                nc.vector.tensor_tensor(out=hi_lo[:], in0=cols[:, 3:6:2], in1=cols[:, 4:7:2], op=ALU.add)
                half_hi = keep.tile([P, 1], F32)
                nc.vector.tensor_scalar(out=half_hi[:], in0=hi_lo[:, 0:1], scalar1=0.5, scalar2=None, op0=ALU.mult)
                nc.vector.tensor_scalar(
                    out=tanh_bias[:], in0=cols[:, 0:MEMBERS], scalar1=half_hi[:, 0:1], scalar2=None, op0=ALU.subtract
                )
                powers = keep.tile([P, 2], F32)
                nc.vector.tensor_scalar(out=powers[:], in0=hi_lo[:], scalar1=math.log2(math.e), scalar2=None, op0=ALU.mult)
                two = keep.tile([P, 2], F32)
                nc.gpsimd.memset(two[:], 2.0)
                exp_hi_lo = keep.tile([P, 2], F32)
                nc.gpsimd.tensor_tensor(out=exp_hi_lo[:], in0=two[:], in1=powers[:], op=ALU.pow)
                nc.gpsimd.tensor_scalar(
                    out=sqrt_scale[:], in0=exp_hi_lo[:, 0:1], scalar1=0.5, scalar2=None, op0=ALU.mult
                )
                nc.gpsimd.tensor_tensor(out=sqrt_bias[:], in0=sqrt_scale[:], in1=exp_hi_lo[:, 1:2], op=ALU.add)
                nc.vector.tensor_copy(out=bmu_f32[:], in_=bmu_bf[:])

            nc.vector.tensor_copy(out=bh_cols[:], in_=bh_bf[:])
            regroup_wh(0)
            for i in range(ROUNDS + G_LAG - 1):
                new_step(i)
                run(tanh_sigma, i - G_LAG - 2)
                run(transpose_h, i)
                run(interleave_g, i - G_LAG)
                run(regroup_h, i)
                run(add_bmu, i - G_LAG - 2)
                quantise(i)
                run(layer_1, i - 1)
                if i < ROUNDS:
                    run(swish, i - 1)
                run(heads, i - G_LAG - 1)
                if i + AHEAD < ROUNDS:
                    load_h(i + AHEAD)
                if i in (0, 1):
                    regroup_wh(i + 1)
                if i == 2:
                    prepare_constants()
                if i == ROUNDS:
                    for blocks in HALVES:
                        swish(ROUNDS - 1, blocks)
            r = ROUNDS - 1
            new_step(r + G_LAG)
            interleave_g(r, HALVES[0])
            heads(r - 1)
            tanh_sigma(r - 2)
            interleave_g(r, HALVES[1])
            tanh_sigma(r - 1)
            for blocks in HALVES:
                quantise_last_g(blocks)
                heads(r, blocks)
                tanh_sigma(r, blocks)
            for late in (r - 2, r - 1, r):
                add_bmu(late)

        with tc.psum_pool(name="psum_sg", bufs=4) as psum_sg:
            for first in range(0, BLOCKS, SQRT_BLOCKS):
                blocks = slice(first, first + SQRT_BLOCKS)
                sgT = work.tile([P, SQRT_BLOCKS, P], F32, bufs=3)
                nc.scalar.activation(
                    out=sgT[:],
                    in_=tanh_all[:, blocks, :],
                    func=ACT.Sqrt,
                    bias=sqrt_bias[:, 0:1],
                    scale=sqrt_scale[:, 0:1],
                )
                sg_ps = psum_sg.tile([P, SQRT_BLOCKS, OUT], F32)
                for g in range(SQRT_BLOCKS):
                    nc.tensor.transpose(out=sg_ps[:, g, :], in_=sgT[:, g, :], identity=ident[:])
                width = STORE_BLOCKS if STORE_BLOCKS <= first < BLOCKS - STORE_BLOCKS else SQRT_BLOCKS
                copy = nc.vector.tensor_copy if first < BLOCKS - SQRT_BLOCKS else nc.scalar.copy
                part = first % width
                if part == 0:
                    sg_state = results.tile([P, STORE_BLOCKS, STATE], F32, bufs=6)
                copy(out=sg_state[:, part : part + SQRT_BLOCKS, :], in_=sg_ps[:, :, 0:STATE])
                copy(out=sg_reward[:, blocks, :], in_=sg_ps[:, :, STATE:OUT])
                if blocks.stop % width == 0:
                    nc.sync.dma_start(out=ds_sg[:, blocks.stop - width : blocks.stop, :], in_=sg_state[:, 0:width, :])
                if blocks.stop % REWARD_BLOCKS == 0:
                    stored = slice(blocks.stop - REWARD_BLOCKS, blocks.stop)
                    nc.sync.dma_start(out=r_sg[:, stored, :], in_=sg_reward[:, stored, :])
